import numpy as np
import ml_dtypes


def mxq(x, axis, fmt="e4m3"):
    dtype, down = {"e4m3": (ml_dtypes.float8_e4m3fn, 7), "e5m2": (ml_dtypes.float8_e5m2, 14)}[fmt]
    v = np.moveaxis(np.asarray(x, np.float32).astype(ml_dtypes.bfloat16).astype(np.float64), axis, -1)
    blocks = v.reshape(v.shape[:-1] + (-1, 32))
    amax = np.abs(blocks).max(-1, keepdims=True)
    byte = np.maximum(np.where(amax > 0, np.frexp(amax)[1] - 1 + 127, 0) - down, 1)
    scale = np.exp2(byte - 127.0)
    codes = (blocks / scale).astype(np.float32).astype(dtype).astype(np.float64)
    return np.moveaxis((codes * scale).reshape(v.shape), -1, axis)


BF16 = ml_dtypes.bfloat16


def bf(x):
    return np.asarray(x, np.float32).astype(BF16)


def f64(x):
    return np.asarray(x).astype(np.float64)


B, T, IN, OUT, S = 4, 128, 4096, 4096, 512
N = B * T


def uni(shape):
    return np.random.uniform(0.1, 1.0, shape)


def setup_inputs():
    cv = 12.0 / np.sqrt(IN)
    cr = 1.0 / np.sqrt(S)
    return {
        "x": bf(np.random.standard_normal((B, T, IN))),
        "V": bf(np.random.standard_normal((S, IN)) * 0.02),
        "U": bf(np.random.standard_normal((OUT, S)) * 0.02),
        "v1": bf(uni((1, S)) * cr),
        "v2": bf(uni((1, IN)) * cv),
        "u1": bf(uni((1, OUT))),
        "u2": bf(uni((1, S))),
        "V_R": bf(np.random.standard_normal((S, IN)) * 0.02),
        "U_R": bf(np.random.standard_normal((OUT, S)) * 0.02),
        "v1_R": bf(uni((1, S)) * cr),
        "v2_R": bf(uni((1, IN)) * cv),
        "u1_R": bf(uni((1, OUT))),
        "u2_R": bf(uni((1, S))),
        "bias": bf(np.random.standard_normal(OUT) * 0.5),
    }


def branch(x2, V, U, v1, v2, u1, u2):
    Vq = np.sign(V)
    Uq = np.sign(U)
    h = mxq(x2 * v2, 1, "e4m3") @ mxq(Vq, 1, "e4m3").T
    h = h * (v1 * u2)
    y = mxq(h, 1, "e4m3") @ mxq(Uq, 1, "e4m3").T
    return y * u1


def reference(x, V, U, v1, v2, u1, u2, V_R, U_R, v1_R, v2_R, u1_R, u2_R, bias):
    x2 = f64(x).reshape(N, IN)
    y = branch(x2, f64(V), f64(U), f64(v1), f64(v2), f64(u1), f64(u2))
    y = y + branch(x2, f64(V_R), f64(U_R), f64(v1_R), f64(v2_R), f64(u1_R), f64(u2_R))
    y = y + f64(bias)
    return y.reshape(B, T, OUT)

@@ -1,0 +1,349 @@
+from contextlib import ExitStack
+
+import concourse.mybir as mybir
+from concourse.masks import make_identity
+
+F32 = mybir.dt.float32
+BF16 = mybir.dt.bfloat16
+U32 = mybir.dt.uint32
+U8 = mybir.dt.uint8
+FP8X4 = mybir.dt.float8_e4m3fn_x4
+ACT = mybir.ActivationFunctionType
+ALU = mybir.AluOpType
+
+FLOPS = 2 * 2 * 2 * 512 * 4096 * 512
+
+P = 128
+MANUAL = True
+LOOK = 2
+RAW_BUFS = 8
+LE = 4
+LO = 9
+LM1 = 4
+LH = 1
+
+
+def tile_littlebitlinear_pa_kernel(
+    tc, x, V, U, v1, v2, u1, u2, V_R, U_R, v1_R, v2_R, u1_R, u2_R, bias, out
+):
+    nc = tc.nc
+    x_view = x.flatten_outer_dims().rearrange("(i p) k -> p i k", p=P)
+    out_rows = out.flatten_outer_dims()
+    v_views = [m.rearrange("(u p e) k -> u p e k", u=2, p=P, e=2) for m in (V, V_R)]
+    u_views = [m.rearrange("(a p e) s -> p a (e s)", p=P, e=2) for m in (U, U_R)]
+
+    with ExitStack() as ctx:
+        const = ctx.enter_context(tc.tile_pool(name="const", bufs=1))
+        rawp = ctx.enter_context(tc.tile_pool(name="rawp", bufs=RAW_BUFS))
+        w3 = ctx.enter_context(tc.tile_pool(name="w3", bufs=3))
+        c4 = ctx.enter_context(tc.tile_pool(name="c4", bufs=4))
+        c6 = ctx.enter_context(tc.tile_pool(name="c6", bufs=6))
+        r8 = ctx.enter_context(tc.tile_pool(name="r8", bufs=8))
+        tpp = ctx.enter_context(tc.psum_pool(name="tpp", bufs=3))
+        bkp = ctx.enter_context(tc.psum_pool(name="bkp", bufs=1))
+        if MANUAL:
+            ctx.enter_context(tc.manual_schedule())
+
+        ident = const.tile([P, P], F32, name="ident")
+        sva = const.tile([P, 256], BF16, name="sva")
+        svb = const.tile([P, 256], BF16, name="svb")
+        v2g = const.tile([P, 32], F32, name="v2g")
+        cols = const.tile([P, 112], F32, name="cols")
+        cs = const.tile([P, 8], F32, name="cs")
+        xtg = [const.tile([P, 1024], F32, name="xtg%d" % c) for c in range(8)]
+        gp = [const.tile([P, 4, 512], BF16, name="gp%d" % b) for b in range(2)]
+        gg = [const.tile([P, 2048], BF16, name="gg%d" % b, align_bytes=64) for b in range(2)]
+        gc = [const.tile([P, 512], U32, name="gc%d" % b, align_bytes=64) for b in range(2)]
+        gs = [const.tile([P, 512], U8, name="gs%d" % b, align_bytes=64) for b in range(2)]
+
+        nc.vector.memset(sva[:].bitcast(F32), 0.0)
+        nc.vector.memset(svb[:].bitcast(F32), 0.0)
+        make_identity(nc, ident[:])
+
+        def small(dst, row, vec, rows):
+            nc.sync.dma_start(out=dst[row : row + rows, :], in_=vec)
+
+        small(sva, 0, v2.rearrange("o (r c) -> (o r) c", c=256), 16)
+        small(sva, 16, v2_R.rearrange("o (r c) -> (o r) c", c=256), 16)
+
+        chunks = []
+        for q in range(4):
+            chunks.extend([("x", 0, q), ("v", 0, q)])
+        for q in range(4):
+            chunks.append(("v", 1, q))
+        for q in range(4):
+            chunks.extend([("u", 0, q), ("u", 1, q)])
+        raw = {}
+        n_loaded = [0]
+
+        def load_piece(key, lo, hi):
+            kind, b, q = key
+            t3 = raw[key][:].rearrange("p (i k) -> p i k", i=4)
+            if hi - lo == 512:
+                t3 = raw[key][:, 4 * lo : 4 * lo + 2048].rearrange("p (i k) -> p i k", i=4)
+                src_lo = 1024 * q + lo
+                if kind == "x":
+                    nc.sync.dma_start(out=t3, in_=x_view[:, :, src_lo : src_lo + 512])
+                else:
+                    for u in range(2):
+                        nc.sync.dma_start(out=t3[:, 2 * u : 2 * u + 2, :], in_=v_views[b][u][:, :, src_lo : src_lo + 512])
+            else:
+                if kind == "x":
+                    nc.sync.dma_start(out=t3[:, :, lo:hi], in_=x_view[:, :, 1024 * q + lo : 1024 * q + hi])
+                elif kind == "v":
+                    for u in range(2):
+                        nc.sync.dma_start(
+                            out=t3[:, 2 * u : 2 * u + 2, lo:hi],
+                            in_=v_views[b][u][:, :, 1024 * q + lo : 1024 * q + hi],
+                        )
+                else:
+                    nc.sync.dma_start(out=t3, in_=u_views[b][:, 4 * q : 4 * q + 4, :])
+
+        def load_next(pieces=1):
+            j = n_loaded[0]
+            if j >= len(chunks):
+                return
+            n_loaded[0] = j + 1
+            raw[chunks[j]] = rawp.tile([P, 4096], BF16, name="raw")
+            if pieces == 1:
+                load_piece(chunks[j], 0, 1024)
+
+        load_next(2)
+        load_next(2)
+        for lo in (0, 512):
+            load_piece(chunks[0], lo, lo + 512)
+            load_piece(chunks[1], lo, lo + 512)
+        for extra in range(RAW_BUFS - 2):
+            load_next()
+        small(svb, 0, u1.rearrange("o (r c) -> (o r) c", c=256), 16)
+        small(svb, 16, u1_R.rearrange("o (r c) -> (o r) c", c=256), 16)
+        small(svb, 32, bias.rearrange("(r c) -> r c", c=256), 16)
+        small(svb, 48, v1.rearrange("o (r c) -> (o r) c", c=256), 2)
+        small(svb, 50, u2.rearrange("o (r c) -> (o r) c", c=256), 2)
+        small(svb, 52, v1_R.rearrange("o (r c) -> (o r) c", c=256), 2)
+        small(svb, 54, u2_R.rearrange("o (r c) -> (o r) c", c=256), 2)
+
+        banks = [("sva", 0, 0)]
+        for c in range(8):
+            banks.extend([("x", c, 0), ("x", c, 1), ("w", c, 0), ("w", c, 1)])
+            if c == 5:
+                banks.append(("svb", 0, 0))
+        for s in range(8, 32):
+            banks.extend([("w", s, 0), ("w", s, 1)])
+
+        later = {}
+
+        def at(slot, fn):
+            if slot not in later:
+                later[slot] = []
+            later[slot].append(fn)
+
+        tp = {}
+        wg = {}
+        xvg = {}
+        xcode = {}
+        wcode = {}
+        acc = {}
+        res = {}
+        counters = {"y": 0, "ot": 0}
+
+        def fill(n):
+            kind, a, h = banks[n]
+            bank = tpp.tile([P, 512], F32, name="tp")
+            tp[n] = bank
+            if kind == "sva" or kind == "svb":
+                src = sva if kind == "sva" else svb
+                nc.tensor.transpose(out=bank[:, 0:P], in_=src[:].bitcast(F32), identity=ident[:])
+                return
+            if kind == "x":
+                key = ("x", 0, a // 2)
+            elif a < 16:
+                key = ("v", a // 8, (a % 8) // 2)
+            else:
+                key = ("u", a % 2, (2 * ((a - 16) // 2) + h) // 4)
+            words = raw[key][:].bitcast(F32)
+            for u in range(2):
+                for j in range(2):
+                    if a < 2:
+                        col = (a % 2) * 1024 + (2 * h + j) * 256 + u * P
+                    elif kind == "x" or a < 16:
+                        col = (2 * h + j) * 512 + (a % 2) * 256 + u * P
+                    else:
+                        col = ((2 * ((a - 16) // 2) + h) % 4) * 512 + j * 256 + u * P
+                    nc.tensor.transpose(
+                        out=bank[:, u * 256 + j * P : u * 256 + (j + 1) * P],
+                        in_=words[:, col : col + P],
+                        identity=ident[:],
+                    )
+            if h == 1:
+                if kind == "x" or a < 16:
+                    if a % 2 == 1:
+                        load_next()
+                elif ((a - 16) // 2) % 2 == 1:
+                    load_next()
+
+        def quant(src, name, pool):
+            codes = pool.tile([P, 512], U32, name=name + "c", align_bytes=64)
+            scales = pool.tile([P, 512], U8, name=name + "s", align_bytes=64)
+            nc.vector.quantize_mx(out=codes[:].bitcast(FP8X4), scales=scales[:], in_=src)
+            return (codes, scales)
+
+        def mul_x(j):
+            b, c = j // 8, j % 8
+            t = w3.tile([P, 2048], BF16, name="xvg", align_bytes=64)
+            xvg[j] = t
+            nc.vector.tensor_tensor(
+                out=t[:].rearrange("p (n t) -> p n t", t=4),
+                in0=xtg[c][:].bitcast(BF16).rearrange("p (n t) -> p n t", t=4),
+                in1=v2g[:].bitcast(BF16)[:, 32 * b + 4 * c : 32 * b + 4 * c + 4].unsqueeze(1).to_broadcast([P, 512, 4]),
+                op=ALU.mult,
+            )
+
+        def quant_x(j):
+            xcode[j] = quant(xvg[j][:], "x", c4)
+
+        def quant_w(s):
+            wcode[s] = quant(wg[s][:], "w" if s < 16 else "u", c4 if s < 16 else c6)
+
+        def mm1(j):
+            b, c = j // 8, j % 8
+            for t in range(4):
+                if c == 0:
+                    acc[(b, t)] = bkp.tile([P, 512], F32, name="b%d" % t)
+                nc.tensor.matmul_mx(
+                    out=acc[(b, t)][:],
+                    lhsT=wcode[j][0][:, t * P : (t + 1) * P].bitcast(FP8X4),
+                    lhsT_scale=wcode[j][1][:, t * P : (t + 1) * P],
+                    rhs=xcode[j][0][:].bitcast(FP8X4),
+                    rhs_scale=xcode[j][1][:],
+                    start=(c == 0),
+                    stop=(c == 7),
+                )
+
+        def h_exit(b, t):
+            if t % 2 == 0:
+                nc.scalar.activation(out=gp[b][:, t, :], in_=acc[(b, t)][:], func=ACT.Copy, scale=cs[:, 4 * b + t : 4 * b + t + 1])
+            else:
+                nc.vector.tensor_scalar(
+                    out=gp[b][:, t, :], in0=acc[(b, t)][:], scalar1=cs[:, 4 * b + t : 4 * b + t + 1], scalar2=None, op0=ALU.mult
+                )
+
+        def regroup_g(b):
+            nc.vector.tensor_copy(out=gg[b][:].rearrange("p (n t) -> p n t", t=4), in_=gp[b][:].rearrange("p t n -> p n t"))
+
+        def quant_g(b):
+            nc.vector.quantize_mx(out=gc[b][:].bitcast(FP8X4), scales=gs[b][:], in_=gg[b][:])
+
+        def stage2(g, t, drain_phase):
+            ys = []
+            for b in range(2):
+                y = bkp.tile([P, 512], F32, name="b%d" % (counters["y"] % 3))
+                counters["y"] = counters["y"] + 1
+                codes, scales = wcode[16 + 2 * g + b]
+                nc.tensor.matmul_mx(
+                    out=y[:],
+                    lhsT=codes[:, t * P : (t + 1) * P].bitcast(FP8X4),
+                    lhsT_scale=scales[:, t * P : (t + 1) * P],
+                    rhs=gc[b][:].bitcast(FP8X4),
+                    rhs_scale=gs[b][:],
+                    start=True,
+                    stop=True,
+                )
+                ys.append(y)
+            k = 4 * g + t
+            t1 = w3.tile([P, 512], F32, name="t1")
+            if t == 3 and not drain_phase:
+                nc.vector.tensor_scalar(
+                    out=t1[:], in0=ys[0][:], scalar1=cols[:, k : k + 1], scalar2=cols[:, 64 + k : 65 + k], op0=ALU.mult, op1=ALU.add
+                )
+            else:
+                nc.scalar.activation(
+                    out=t1[:], in_=ys[0][:], func=ACT.Identity, scale=cols[:, k : k + 1], bias=cols[:, 64 + k : 65 + k]
+                )
+            r = r8.tile([P, 512], F32, name="res")
+            res[(g, t)] = r
+            nc.vector.scalar_tensor_tensor(
+                out=r[:], in0=ys[1][:], scalar=cols[:, 32 + k : 33 + k], in1=t1[:], op0=ALU.mult, op1=ALU.add
+            )
+
+        def finish(g, i, drain_phase):
+            ot = bkp.tile([P, 512], F32, name="b%d" % (3 + counters["ot"] % 2))
+            counters["ot"] = counters["ot"] + 1
+            for t in range(4):
+                nc.tensor.transpose(out=ot[:, t * P : (t + 1) * P], in_=res[(g, t)][:, i * P : (i + 1) * P], identity=ident[:])
+            ob = c4.tile([P, 512], F32, name="ob")
+            dst = ob[:].rearrange("p (h m e) -> p h m e", h=2, e=2)
+            src = ot[:].rearrange("p (h e m) -> p h m e", h=2, e=2)
+            if drain_phase:
+                nc.scalar.copy(out=dst, in_=src)
+            else:
+                nc.vector.tensor_copy(out=dst, in_=src)
+            nc.sync.dma_start(out=out_rows[i * P : (i + 1) * P, g * 512 : (g + 1) * 512], in_=ob[:])
+
+        def step_v(j, n):
+            if j > 0:
+                quant_x(j - 1)
+            if j < 16:
+                mul_x(j)
+            if j > 0:
+                quant_w(j - 1)
+                at(n + LM1, lambda: mm1(j - 1))
+            if j - 1 == 7 or j - 1 == 15:
+                b = (j - 1) // 8
+                at(n + LM1 + LH, lambda: [h_exit(b, t) for t in range(4)])
+                at(n + LM1 + LH + 1, lambda: regroup_g(b))
+                at(n + LM1 + LH + 2, lambda: quant_g(b))
+
+        def drain(n):
+            kind, a, h = banks[n]
+            bank = tp[n]
+            if kind == "sva":
+                nc.vector.tensor_copy(out=v2g[:], in_=bank[:, 0:32])
+            elif kind == "svb":
+                nc.vector.tensor_copy(out=cols[:], in_=bank[:, 0:56].bitcast(BF16))
+                for b in range(2):
+                    nc.vector.tensor_tensor(
+                        out=cs[:, 4 * b : 4 * b + 4],
+                        in0=cols[:, 96 + 8 * b : 100 + 8 * b],
+                        in1=cols[:, 100 + 8 * b : 104 + 8 * b],
+                        op=ALU.mult,
+                    )
+            elif kind == "x":
+                dst = xtg[a][:, h * 512 : (h + 1) * 512].rearrange("p (n u) -> p n u", u=2)
+                src = bank[:].rearrange("p (u n) -> p n u", u=2)
+                if h == 0:
+                    nc.scalar.copy(out=dst, in_=src)
+                else:
+                    nc.vector.tensor_copy(out=dst, in_=src)
+                    step_v(a, n)
+            else:
+                if h == 0:
+                    wg[a] = w3.tile([P, 2048], BF16, name="wg", align_bytes=64)
+                nc.scalar.activation(
+                    out=wg[a][:, h * 1024 : (h + 1) * 1024].rearrange("p (c u e) -> p c u e", u=2, e=2),
+                    in_=bank[:].bitcast(BF16).rearrange("p (u c e) -> p c u e", u=2, e=2),
+                    func=ACT.Sign,
+                )
+                if h == 0 and 8 <= a <= 16:
+                    step_v(a, n)
+                if a > 16 and h == 0:
+                    quant_w(a - 1)
+                if a >= 17 and a % 2 == 1 and h == 1:
+                    g = (a - 17) // 2
+                    last = a == 31
+                    if last:
+                        at(n + 1, lambda: quant_w(31))
+                    for t in range(4):
+                        at(n + LE + t, lambda t=t: stage2(g, t, last))
+                        at(n + LO + t, lambda t=t: finish(g, t, g >= 6))
+
+        n_banks = len(banks)
+        for n in range(LOOK):
+            fill(n)
+        for n in range(n_banks + LO + 5):
+            if n + LOOK < n_banks:
+                fill(n + LOOK)
+            if n < n_banks:
+                drain(n)
+            for fn in later.get(n, []):
+                fn()

@@ -14,7 +14,7 @@ ALU = mybir.AluOpType
 FLOPS = 2 * 2 * 2 * 512 * 4096 * 512
 
 P = 128
-MANUAL = True
+MANUAL = False
 LOOK = 2
 RAW_BUFS = 8
 LE = 4

@@ -14,13 +14,16 @@ ALU = mybir.AluOpType
 FLOPS = 2 * 2 * 2 * 512 * 4096 * 512
 
 P = 128
-MANUAL = False
-LOOK = 2
-RAW_BUFS = 8
-LE = 4
-LO = 9
-LM1 = 4
-LH = 1
+RAW_BUFS = 16
+MANUAL = 1
+DA = 4
+DB = 5
+D1 = 5
+D2 = 6
+DO = 10
+D3 = 11
+V_E1 = 3
+S_E3_FROM = 33
 
 
 def tile_littlebitlinear_pa_kernel(
@@ -35,12 +38,13 @@ def tile_littlebitlinear_pa_kernel(
     with ExitStack() as ctx:
         const = ctx.enter_context(tc.tile_pool(name="const", bufs=1))
         rawp = ctx.enter_context(tc.tile_pool(name="rawp", bufs=RAW_BUFS))
-        w3 = ctx.enter_context(tc.tile_pool(name="w3", bufs=3))
-        c4 = ctx.enter_context(tc.tile_pool(name="c4", bufs=4))
-        c6 = ctx.enter_context(tc.tile_pool(name="c6", bufs=6))
-        r8 = ctx.enter_context(tc.tile_pool(name="r8", bufs=8))
-        tpp = ctx.enter_context(tc.psum_pool(name="tpp", bufs=3))
-        bkp = ctx.enter_context(tc.psum_pool(name="bkp", bufs=1))
+        three = ctx.enter_context(tc.tile_pool(name="three", bufs=3))
+        four = ctx.enter_context(tc.tile_pool(name="four", bufs=4))
+        eight = ctx.enter_context(tc.tile_pool(name="eight", bufs=8))
+        sixteen = ctx.enter_context(tc.tile_pool(name="sixteen", bufs=16))
+        wp = ctx.enter_context(tc.psum_pool(name="wp", bufs=2))
+        xo = ctx.enter_context(tc.psum_pool(name="xo", bufs=2))
+        accp = ctx.enter_context(tc.psum_pool(name="accp", bufs=4))
         if MANUAL:
             ctx.enter_context(tc.manual_schedule())
 
@@ -50,257 +54,259 @@ def tile_littlebitlinear_pa_kernel(
         v2g = const.tile([P, 32], F32, name="v2g")
         cols = const.tile([P, 112], F32, name="cols")
         cs = const.tile([P, 8], F32, name="cs")
-        xtg = [const.tile([P, 1024], F32, name="xtg%d" % c) for c in range(8)]
-        gp = [const.tile([P, 4, 512], BF16, name="gp%d" % b) for b in range(2)]
-        gg = [const.tile([P, 2048], BF16, name="gg%d" % b, align_bytes=64) for b in range(2)]
-        gc = [const.tile([P, 512], U32, name="gc%d" % b, align_bytes=64) for b in range(2)]
-        gs = [const.tile([P, 512], U8, name="gs%d" % b, align_bytes=64) for b in range(2)]
 
         nc.vector.memset(sva[:].bitcast(F32), 0.0)
         nc.vector.memset(svb[:].bitcast(F32), 0.0)
         make_identity(nc, ident[:])
 
-        def small(dst, row, vec, rows):
-            nc.sync.dma_start(out=dst[row : row + rows, :], in_=vec)
+        def rows_of(vec):
+            return vec.rearrange("o (r c) -> (o r) c", c=256)
 
-        small(sva, 0, v2.rearrange("o (r c) -> (o r) c", c=256), 16)
-        small(sva, 16, v2_R.rearrange("o (r c) -> (o r) c", c=256), 16)
+        nc.sync.dma_start(out=sva[0:16, :], in_=rows_of(v2))
+        nc.sync.dma_start(out=sva[16:32, :], in_=rows_of(v2_R))
 
-        chunks = []
-        for q in range(4):
-            chunks.extend([("x", 0, q), ("v", 0, q)])
-        for q in range(4):
-            chunks.append(("v", 1, q))
-        for q in range(4):
-            chunks.extend([("u", 0, q), ("u", 1, q)])
-        raw = {}
-        n_loaded = [0]
-
-        def load_piece(key, lo, hi):
-            kind, b, q = key
-            t3 = raw[key][:].rearrange("p (i k) -> p i k", i=4)
-            if hi - lo == 512:
-                t3 = raw[key][:, 4 * lo : 4 * lo + 2048].rearrange("p (i k) -> p i k", i=4)
-                src_lo = 1024 * q + lo
-                if kind == "x":
-                    nc.sync.dma_start(out=t3, in_=x_view[:, :, src_lo : src_lo + 512])
-                else:
-                    for u in range(2):
-                        nc.sync.dma_start(out=t3[:, 2 * u : 2 * u + 2, :], in_=v_views[b][u][:, :, src_lo : src_lo + 512])
-            else:
-                if kind == "x":
-                    nc.sync.dma_start(out=t3[:, :, lo:hi], in_=x_view[:, :, 1024 * q + lo : 1024 * q + hi])
-                elif kind == "v":
-                    for u in range(2):
-                        nc.sync.dma_start(
-                            out=t3[:, 2 * u : 2 * u + 2, lo:hi],
-                            in_=v_views[b][u][:, :, 1024 * q + lo : 1024 * q + hi],
-                        )
-                else:
-                    nc.sync.dma_start(out=t3, in_=u_views[b][:, 4 * q : 4 * q + 4, :])
-
-        def load_next(pieces=1):
-            j = n_loaded[0]
-            if j >= len(chunks):
-                return
-            n_loaded[0] = j + 1
-            raw[chunks[j]] = rawp.tile([P, 4096], BF16, name="raw")
-            if pieces == 1:
-                load_piece(chunks[j], 0, 1024)
-
-        load_next(2)
-        load_next(2)
-        for lo in (0, 512):
-            load_piece(chunks[0], lo, lo + 512)
-            load_piece(chunks[1], lo, lo + 512)
-        for extra in range(RAW_BUFS - 2):
-            load_next()
-        small(svb, 0, u1.rearrange("o (r c) -> (o r) c", c=256), 16)
-        small(svb, 16, u1_R.rearrange("o (r c) -> (o r) c", c=256), 16)
-        small(svb, 32, bias.rearrange("(r c) -> r c", c=256), 16)
-        small(svb, 48, v1.rearrange("o (r c) -> (o r) c", c=256), 2)
-        small(svb, 50, u2.rearrange("o (r c) -> (o r) c", c=256), 2)
-        small(svb, 52, v1_R.rearrange("o (r c) -> (o r) c", c=256), 2)
-        small(svb, 54, u2_R.rearrange("o (r c) -> (o r) c", c=256), 2)
-
-        banks = [("sva", 0, 0)]
+        order = []
         for c in range(8):
-            banks.extend([("x", c, 0), ("x", c, 1), ("w", c, 0), ("w", c, 1)])
-            if c == 5:
-                banks.append(("svb", 0, 0))
-        for s in range(8, 32):
-            banks.extend([("w", s, 0), ("w", s, 1)])
+            order.extend([("x", 0, c), ("v", 0, c)])
+        order.extend([("v", 1, c) for c in range(8)])
+        for grp in range(8):
+            order.extend([("u", 0, grp), ("u", 1, grp)])
+        raw = {}
 
-        later = {}
+        def load_next():
+            if len(raw) == len(order):
+                return
+            kind, b, j = order[len(raw)]
+            t = rawp.tile([P, 2048], BF16, name="raw")
+            raw[(kind, b, j)] = t
+            t3 = t[:].rearrange("p (r k) -> p r k", r=4)
+            if kind == "x":
+                nc.sync.dma_start(out=t3, in_=x_view[:, :, 512 * j : 512 * (j + 1)])
+            elif kind == "v":
+                for u in range(2):
+                    nc.sync.dma_start(out=t3[:, 2 * u : 2 * u + 2, :], in_=v_views[b][u][:, :, 512 * j : 512 * (j + 1)])
+            else:
+                nc.sync.dma_start(out=t[:].rearrange("p (a k) -> p a k", a=2), in_=u_views[b][:, 2 * j : 2 * j + 2, :])
 
-        def at(slot, fn):
-            if slot not in later:
-                later[slot] = []
-            later[slot].append(fn)
+        for first in range(RAW_BUFS):
+            load_next()
+        nc.sync.dma_start(out=svb[0:16, :], in_=rows_of(u1))
+        nc.sync.dma_start(out=svb[16:32, :], in_=rows_of(u1_R))
+        nc.sync.dma_start(out=svb[32:48, :], in_=bias.rearrange("(r c) -> r c", c=256))
+        nc.sync.dma_start(out=svb[48:50, :], in_=rows_of(v1))
+        nc.sync.dma_start(out=svb[50:52, :], in_=rows_of(u2))
+        nc.sync.dma_start(out=svb[52:54, :], in_=rows_of(v1_R))
+        nc.sync.dma_start(out=svb[54:56, :], in_=rows_of(u2_R))
 
-        tp = {}
+        def w_key(j):
+            return ("v", j // 8, j % 8) if j < 16 else ("u", j % 2, (j - 16) // 2)
+
+        def u_bank(s):
+            return (16 + 2 * (s // 4) + s % 2, (s % 4) // 2)
+
+        bank = {}
+        xt = {}
+        xv = {}
         wg = {}
-        xvg = {}
         xcode = {}
         wcode = {}
         acc = {}
+        gcode = {}
+        gp = {}
+        gg = {}
+        ya = {}
+        yb = {}
+        t1 = {}
         res = {}
-        counters = {"y": 0, "ot": 0}
+        ot = {}
 
-        def fill(n):
-            kind, a, h = banks[n]
-            bank = tpp.tile([P, 512], F32, name="tp")
-            tp[n] = bank
-            if kind == "sva" or kind == "svb":
-                src = sva if kind == "sva" else svb
-                nc.tensor.transpose(out=bank[:, 0:P], in_=src[:].bitcast(F32), identity=ident[:])
-                return
-            if kind == "x":
-                key = ("x", 0, a // 2)
-            elif a < 16:
-                key = ("v", a // 8, (a % 8) // 2)
-            else:
-                key = ("u", a % 2, (2 * ((a - 16) // 2) + h) // 4)
+        def fill(key, h, pool, name):
+            b = pool.tile([P, 512], F32, name=name)
+            bank[(key, h)] = b
             words = raw[key][:].bitcast(F32)
             for u in range(2):
                 for j in range(2):
-                    if a < 2:
-                        col = (a % 2) * 1024 + (2 * h + j) * 256 + u * P
-                    elif kind == "x" or a < 16:
-                        col = (2 * h + j) * 512 + (a % 2) * 256 + u * P
-                    else:
-                        col = ((2 * ((a - 16) // 2) + h) % 4) * 512 + j * 256 + u * P
-                    nc.tensor.transpose(
-                        out=bank[:, u * 256 + j * P : u * 256 + (j + 1) * P],
-                        in_=words[:, col : col + P],
-                        identity=ident[:],
-                    )
+                    col = (2 * h + j) * 256 + u * P
+                    nc.tensor.transpose(out=b[:, u * 256 + j * P : u * 256 + (j + 1) * P], in_=words[:, col : col + P], identity=ident[:])
             if h == 1:
-                if kind == "x" or a < 16:
-                    if a % 2 == 1:
-                        load_next()
-                elif ((a - 16) // 2) % 2 == 1:
-                    load_next()
+                load_next()
 
-        def quant(src, name, pool):
-            codes = pool.tile([P, 512], U32, name=name + "c", align_bytes=64)
-            scales = pool.tile([P, 512], U8, name=name + "s", align_bytes=64)
-            nc.vector.quantize_mx(out=codes[:].bitcast(FP8X4), scales=scales[:], in_=src)
-            return (codes, scales)
+        def fill_u(s):
+            if s < 32:
+                fill(w_key(u_bank(s)[0]), u_bank(s)[1], wp, "wp")
 
-        def mul_x(j):
-            b, c = j // 8, j % 8
-            t = w3.tile([P, 2048], BF16, name="xvg", align_bytes=64)
-            xvg[j] = t
-            nc.vector.tensor_tensor(
-                out=t[:].rearrange("p (n t) -> p n t", t=4),
-                in0=xtg[c][:].bitcast(BF16).rearrange("p (n t) -> p n t", t=4),
-                in1=v2g[:].bitcast(BF16)[:, 32 * b + 4 * c : 32 * b + 4 * c + 4].unsqueeze(1).to_broadcast([P, 512, 4]),
-                op=ALU.mult,
+        def sign_u(s):
+            j, h = u_bank(s)
+            wg[(j, h)] = four.tile([P, 1024], BF16, name="ug", align_bytes=64)
+            nc.scalar.activation(
+                out=wg[(j, h)][:].rearrange("p (c u e) -> p c u e", u=2, e=2),
+                in_=bank[(w_key(j), h)][:].bitcast(BF16).rearrange("p (u c e) -> p c u e", u=2, e=2),
+                func=ACT.Sign,
             )
 
-        def quant_x(j):
-            xcode[j] = quant(xvg[j][:], "x", c4)
+        def quant_u(s):
+            if 0 <= s < 32:
+                codes = sixteen.tile([P, 256], U32, name="uc", align_bytes=64)
+                scales = sixteen.tile([P, 256], U8, name="us", align_bytes=64)
+                nc.vector.quantize_mx(out=codes[:].bitcast(FP8X4), scales=scales[:], in_=wg[u_bank(s)][:])
+                wcode[u_bank(s)] = (codes, scales)
 
-        def quant_w(s):
-            wcode[s] = quant(wg[s][:], "w" if s < 16 else "u", c4 if s < 16 else c6)
+        def fill_w(j, h):
+            if j < 16:
+                fill(w_key(j), h, wp, "wp")
+            elif j == 16:
+                fill_u(0)
 
-        def mm1(j):
-            b, c = j // 8, j % 8
-            for t in range(4):
-                if c == 0:
-                    acc[(b, t)] = bkp.tile([P, 512], F32, name="b%d" % t)
-                nc.tensor.matmul_mx(
-                    out=acc[(b, t)][:],
-                    lhsT=wcode[j][0][:, t * P : (t + 1) * P].bitcast(FP8X4),
-                    lhsT_scale=wcode[j][1][:, t * P : (t + 1) * P],
-                    rhs=xcode[j][0][:].bitcast(FP8X4),
-                    rhs_scale=xcode[j][1][:],
-                    start=(c == 0),
-                    stop=(c == 7),
-                )
+        def fill_x(c, h):
+            if c < 8:
+                fill(("x", 0, c), h, xo, "xo")
 
-        def h_exit(b, t):
-            if t % 2 == 0:
-                nc.scalar.activation(out=gp[b][:, t, :], in_=acc[(b, t)][:], func=ACT.Copy, scale=cs[:, 4 * b + t : 4 * b + t + 1])
-            else:
-                nc.vector.tensor_scalar(
-                    out=gp[b][:, t, :], in0=acc[(b, t)][:], scalar1=cs[:, 4 * b + t : 4 * b + t + 1], scalar2=None, op0=ALU.mult
-                )
-
-        def regroup_g(b):
-            nc.vector.tensor_copy(out=gg[b][:].rearrange("p (n t) -> p n t", t=4), in_=gp[b][:].rearrange("p t n -> p n t"))
-
-        def quant_g(b):
-            nc.vector.quantize_mx(out=gc[b][:].bitcast(FP8X4), scales=gs[b][:], in_=gg[b][:])
-
-        def stage2(g, t, drain_phase):
-            ys = []
-            for b in range(2):
-                y = bkp.tile([P, 512], F32, name="b%d" % (counters["y"] % 3))
-                counters["y"] = counters["y"] + 1
-                codes, scales = wcode[16 + 2 * g + b]
-                nc.tensor.matmul_mx(
-                    out=y[:],
-                    lhsT=codes[:, t * P : (t + 1) * P].bitcast(FP8X4),
-                    lhsT_scale=scales[:, t * P : (t + 1) * P],
-                    rhs=gc[b][:].bitcast(FP8X4),
-                    rhs_scale=gs[b][:],
-                    start=True,
-                    stop=True,
-                )
-                ys.append(y)
-            k = 4 * g + t
-            t1 = w3.tile([P, 512], F32, name="t1")
-            if t == 3 and not drain_phase:
-                nc.vector.tensor_scalar(
-                    out=t1[:], in0=ys[0][:], scalar1=cols[:, k : k + 1], scalar2=cols[:, 64 + k : 65 + k], op0=ALU.mult, op1=ALU.add
-                )
-            else:
-                nc.scalar.activation(
-                    out=t1[:], in_=ys[0][:], func=ACT.Identity, scale=cols[:, k : k + 1], bias=cols[:, 64 + k : 65 + k]
-                )
-            r = r8.tile([P, 512], F32, name="res")
-            res[(g, t)] = r
-            nc.vector.scalar_tensor_tensor(
-                out=r[:], in0=ys[1][:], scalar=cols[:, 32 + k : 33 + k], in1=t1[:], op0=ALU.mult, op1=ALU.add
-            )
-
-        def finish(g, i, drain_phase):
-            ot = bkp.tile([P, 512], F32, name="b%d" % (3 + counters["ot"] % 2))
-            counters["ot"] = counters["ot"] + 1
-            for t in range(4):
-                nc.tensor.transpose(out=ot[:, t * P : (t + 1) * P], in_=res[(g, t)][:, i * P : (i + 1) * P], identity=ident[:])
-            ob = c4.tile([P, 512], F32, name="ob")
-            dst = ob[:].rearrange("p (h m e) -> p h m e", h=2, e=2)
-            src = ot[:].rearrange("p (h e m) -> p h m e", h=2, e=2)
-            if drain_phase:
+        def x_exit(c, h):
+            if h == 0:
+                xt[c] = eight.tile([P, 1024], F32, name="xt")
+            dst = xt[c][:, h * 512 : (h + 1) * 512].rearrange("p (n u) -> p n u", u=2)
+            src = bank[(("x", 0, c), h)][:].rearrange("p (u n) -> p n u", u=2)
+            if h == 0:
                 nc.scalar.copy(out=dst, in_=src)
             else:
                 nc.vector.tensor_copy(out=dst, in_=src)
-            nc.sync.dma_start(out=out_rows[i * P : (i + 1) * P, g * 512 : (g + 1) * 512], in_=ob[:])
 
-        def step_v(j, n):
-            if j > 0:
-                quant_x(j - 1)
+        def sign(j, h):
+            if h == 0:
+                wg[j] = three.tile([P, 2048], BF16, name="wg", align_bytes=64)
+            nc.scalar.activation(
+                out=wg[j][:, h * 1024 : (h + 1) * 1024].rearrange("p (c u e) -> p c u e", u=2, e=2),
+                in_=bank[(w_key(j), h)][:].bitcast(BF16).rearrange("p (u c e) -> p c u e", u=2, e=2),
+                func=ACT.Sign,
+            )
+
+        def quantise(src, pool, name):
+            codes = pool.tile([P, 512], U32, name=name + "c", align_bytes=64)
+            scales = pool.tile([P, 512], U8, name=name + "s", align_bytes=64)
+            nc.vector.quantize_mx(out=codes[:].bitcast(FP8X4), scales=scales[:], in_=src[:])
+            return (codes, scales)
+
+        def quant_w(j):
+            if 0 <= j < 16:
+                wcode[j] = quantise(wg[j], four, "w")
+
+        def mul_x(j):
             if j < 16:
-                mul_x(j)
-            if j > 0:
-                quant_w(j - 1)
-                at(n + LM1, lambda: mm1(j - 1))
-            if j - 1 == 7 or j - 1 == 15:
-                b = (j - 1) // 8
-                at(n + LM1 + LH, lambda: [h_exit(b, t) for t in range(4)])
-                at(n + LM1 + LH + 1, lambda: regroup_g(b))
-                at(n + LM1 + LH + 2, lambda: quant_g(b))
+                b, c = j // 8, j % 8
+                xv[j] = three.tile([P, 2048], BF16, name="xv", align_bytes=64)
+                nc.vector.tensor_tensor(
+                    out=xv[j][:].rearrange("p (n t) -> p n t", t=4),
+                    in0=xt[c][:].bitcast(BF16).rearrange("p (n t) -> p n t", t=4),
+                    in1=v2g[:].bitcast(BF16)[:, 32 * b + 4 * c : 32 * b + 4 * c + 4].unsqueeze(1).to_broadcast([P, 512, 4]),
+                    op=ALU.mult,
+                )
 
-        def drain(n):
-            kind, a, h = banks[n]
-            bank = tp[n]
-            if kind == "sva":
-                nc.vector.tensor_copy(out=v2g[:], in_=bank[:, 0:32])
-            elif kind == "svb":
-                nc.vector.tensor_copy(out=cols[:], in_=bank[:, 0:56].bitcast(BF16))
+        def quant_x(j):
+            if 0 <= j < 16:
+                xcode[j] = quantise(xv[j], four, "x")
+
+        def mx(dst, lhs, t, rhs, start, stop):
+            nc.tensor.matmul_mx(
+                out=dst[:],
+                lhsT=lhs[0][:, t * P : (t + 1) * P].bitcast(FP8X4),
+                lhsT_scale=lhs[1][:, t * P : (t + 1) * P],
+                rhs=rhs[0][:].bitcast(FP8X4),
+                rhs_scale=rhs[1][:],
+                start=start,
+                stop=stop,
+            )
+
+        def stage1(j):
+            if 0 <= j < 16:
+                b, c = j // 8, j % 8
+                for t in range(4):
+                    if c == 0:
+                        acc[(b, t)] = accp.tile([P, 512], F32, name="acc")
+                    mx(acc[(b, t)], wcode[j], t, xcode[j], c == 0, c == 7)
+
+        def h_exit(b, engine):
+            if b not in gp:
+                gp[b] = const.tile([P, 4, 512], BF16, name="gp%d" % b)
+            for t in range(4):
+                scale = cs[:, 4 * b + t : 4 * b + t + 1]
+                if t % 2 == 0 and engine == "s":
+                    nc.scalar.activation(out=gp[b][:, t, :], in_=acc[(b, t)][:], func=ACT.Copy, scale=scale)
+                if t % 2 == 1 and engine == "v":
+                    nc.vector.tensor_scalar(out=gp[b][:, t, :], in0=acc[(b, t)][:], scalar1=scale, scalar2=None, op0=ALU.mult)
+
+        def regroup_g(b):
+            gg[b] = const.tile([P, 2048], BF16, name="gg%d" % b, align_bytes=64)
+            nc.vector.tensor_copy(out=gg[b][:].rearrange("p (n t) -> p n t", t=4), in_=gp[b][:].rearrange("p t n -> p n t"))
+
+        def quant_g(b):
+            gcode[b] = quantise(gg[b], const, "g%d" % b)
+
+        def stage2(q, b):
+            if 0 <= q < 32:
+                y = accp.tile([P, 512], F32, name="acc")
+                (ya if b == 0 else yb)[q] = y
+                mx(y, wcode[(16 + 2 * (q // 4) + b, (q % 4) // 2)], q % 2, gcode[b], True, True)
+
+        def scale_main(q, engine):
+            if 0 <= q < 32 and (engine == "v") == (q % 4 == V_E1):
+                t1[q] = three.tile([P, 512], F32, name="t1")
+                if engine == "v":
+                    nc.vector.tensor_scalar(
+                        out=t1[q][:], in0=ya[q][:], scalar1=cols[:, q : q + 1], scalar2=cols[:, 64 + q : 65 + q], op0=ALU.mult, op1=ALU.add
+                    )
+                else:
+                    nc.scalar.activation(
+                        out=t1[q][:], in_=ya[q][:], func=ACT.Identity, scale=cols[:, q : q + 1], bias=cols[:, 64 + q : 65 + q]
+                    )
+
+        def add_residual(q):
+            if 0 <= q < 32:
+                res[q] = eight.tile([P, 512], F32, name="res")
+                nc.vector.scalar_tensor_tensor(
+                    out=res[q][:], in0=yb[q][:], scalar=cols[:, 32 + q : 33 + q], in1=t1[q][:], op0=ALU.mult, op1=ALU.add
+                )
+
+        def back(q):
+            if 0 <= q < 32:
+                grp, i = q // 4, q % 4
+                ot[q] = xo.tile([P, 512], F32, name="xo")
+                for t in range(4):
+                    nc.tensor.transpose(
+                        out=ot[q][:, t * P : (t + 1) * P], in_=res[4 * grp + t][:, i * P : (i + 1) * P], identity=ident[:]
+                    )
+
+        def store(q, engine):
+            if 0 <= q < 32:
+                grp, i = q // 4, q % 4
+                ob = four.tile([P, 512], F32, name="ob")
+                dst = ob[:].rearrange("p (h m e) -> p h m e", h=2, e=2)
+                src = ot[q][:].rearrange("p (h e m) -> p h m e", h=2, e=2)
+                if engine == "s":
+                    nc.scalar.copy(out=dst, in_=src)
+                else:
+                    nc.vector.tensor_copy(out=dst, in_=src)
+                nc.sync.dma_start(out=out_rows[i * P : (i + 1) * P, grp * 512 : (grp + 1) * 512], in_=ob[:])
+
+        spread_a = xo.tile([P, 512], F32, name="xo")
+        nc.tensor.transpose(out=spread_a[:, 0:P], in_=sva[:].bitcast(F32), identity=ident[:])
+        nc.vector.tensor_copy(out=v2g[:], in_=spread_a[:, 0:32])
+
+        fill_x(0, 0)
+        fill_x(0, 1)
+        fill_w(0, 0)
+        for j in range(16):
+            fill_w(j, 1)
+            stage1(j - 2)
+            if j < 8:
+                x_exit(j, 0)
+                x_exit(j, 1)
+                fill_x(j + 1, 0)
+                fill_x(j + 1, 1)
+            if j == 8:
+                spread_b = xo.tile([P, 512], F32, name="xo")
+                nc.tensor.transpose(out=spread_b[:, 0:P], in_=svb[:].bitcast(F32), identity=ident[:])
+            if j == 9:
+                nc.vector.tensor_copy(out=cols[:], in_=spread_b[:, 0:56].bitcast(BF16))
                 for b in range(2):
                     nc.vector.tensor_tensor(
                         out=cs[:, 4 * b : 4 * b + 4],
@@ -308,42 +314,41 @@ def tile_littlebitlinear_pa_kernel(
                         in1=cols[:, 100 + 8 * b : 104 + 8 * b],
                         op=ALU.mult,
                     )
-            elif kind == "x":
-                dst = xtg[a][:, h * 512 : (h + 1) * 512].rearrange("p (n u) -> p n u", u=2)
-                src = bank[:].rearrange("p (u n) -> p n u", u=2)
-                if h == 0:
-                    nc.scalar.copy(out=dst, in_=src)
-                else:
-                    nc.vector.tensor_copy(out=dst, in_=src)
-                    step_v(a, n)
-            else:
-                if h == 0:
-                    wg[a] = w3.tile([P, 2048], BF16, name="wg", align_bytes=64)
-                nc.scalar.activation(
-                    out=wg[a][:, h * 1024 : (h + 1) * 1024].rearrange("p (c u e) -> p c u e", u=2, e=2),
-                    in_=bank[:].bitcast(BF16).rearrange("p (u c e) -> p c u e", u=2, e=2),
-                    func=ACT.Sign,
-                )
-                if h == 0 and 8 <= a <= 16:
-                    step_v(a, n)
-                if a > 16 and h == 0:
-                    quant_w(a - 1)
-                if a >= 17 and a % 2 == 1 and h == 1:
-                    g = (a - 17) // 2
-                    last = a == 31
-                    if last:
-                        at(n + 1, lambda: quant_w(31))
-                    for t in range(4):
-                        at(n + LE + t, lambda t=t: stage2(g, t, last))
-                        at(n + LO + t, lambda t=t: finish(g, t, g >= 6))
+            quant_x(j - 1)
+            mul_x(j)
+            sign(j, 0)
+            fill_w(j + 1, 0)
+            sign(j, 1)
+            quant_w(j - 1)
+            if j == 9:
+                h_exit(0, "s")
+                h_exit(0, "v")
 
-        n_banks = len(banks)
-        for n in range(LOOK):
-            fill(n)
-        for n in range(n_banks + LO + 5):
-            if n + LOOK < n_banks:
-                fill(n + LOOK)
-            if n < n_banks:
-                drain(n)
-            for fn in later.get(n, []):
-                fn()
+        for s in range(32 + D3 + 4):
+            if s == 0:
+                quant_x(15)
+                quant_w(15)
+            quant_u(s - 1)
+            fill_u(s + 1)
+            back(s - DO)
+            if s == 0:
+                stage1(14)
+            if s == 1:
+                stage1(15)
+                regroup_g(0)
+                quant_g(0)
+            stage2(s - DB, 1)
+            stage2(s - DA, 0)
+            if s < 32:
+                sign_u(s)
+            if s == 2:
+                h_exit(1, "s")
+                h_exit(1, "v")
+            if s == 3:
+                regroup_g(1)
+            if s == 4:
+                quant_g(1)
+            scale_main(s - D1, "s")
+            store(s - D3, "s" if s >= S_E3_FROM else "v")
+            add_residual(s - D2)
+            scale_main(s - D1, "v")

@@ -14,16 +14,17 @@ ALU = mybir.AluOpType
 FLOPS = 2 * 2 * 2 * 512 * 4096 * 512
 
 P = 128
-RAW_BUFS = 16
-MANUAL = 1
-DA = 4
-DB = 5
-D1 = 5
-D2 = 6
-DO = 10
-D3 = 11
-V_E1 = 3
-S_E3_FROM = 33
+STEPS = 16
+TILES = 32
+RAW_TILES = 16
+
+MAIN_PASS = 4
+RESIDUAL_PASS = 5
+SCALE = 5
+ADD = 6
+BACK = 8
+STORE = 9
+LAST_SLOT = TILES - 1 + STORE
 
 
 def tile_littlebitlinear_pa_kernel(
@@ -31,324 +32,340 @@ def tile_littlebitlinear_pa_kernel(
 ):
     nc = tc.nc
     x_view = x.flatten_outer_dims().rearrange("(i p) k -> p i k", p=P)
-    out_rows = out.flatten_outer_dims()
-    v_views = [m.rearrange("(u p e) k -> u p e k", u=2, p=P, e=2) for m in (V, V_R)]
+    out_view = out.flatten_outer_dims().rearrange("(i p) o -> p i o", p=P)
+    v_views = [m.rearrange("(a p e) k -> a p e k", a=2, p=P, e=2) for m in (V, V_R)]
     u_views = [m.rearrange("(a p e) s -> p a (e s)", p=P, e=2) for m in (U, U_R)]
 
     with ExitStack() as ctx:
         const = ctx.enter_context(tc.tile_pool(name="const", bufs=1))
-        rawp = ctx.enter_context(tc.tile_pool(name="rawp", bufs=RAW_BUFS))
+        raw_pool = ctx.enter_context(tc.tile_pool(name="raw_pool", bufs=RAW_TILES))
         three = ctx.enter_context(tc.tile_pool(name="three", bufs=3))
         four = ctx.enter_context(tc.tile_pool(name="four", bufs=4))
         eight = ctx.enter_context(tc.tile_pool(name="eight", bufs=8))
         sixteen = ctx.enter_context(tc.tile_pool(name="sixteen", bufs=16))
-        wp = ctx.enter_context(tc.psum_pool(name="wp", bufs=2))
-        xo = ctx.enter_context(tc.psum_pool(name="xo", bufs=2))
-        accp = ctx.enter_context(tc.psum_pool(name="accp", bufs=4))
-        if MANUAL:
-            ctx.enter_context(tc.manual_schedule())
+        weight_banks = ctx.enter_context(tc.psum_pool(name="weight_banks", bufs=2))
+        turn_banks = ctx.enter_context(tc.psum_pool(name="turn_banks", bufs=2))
+        sum_banks = ctx.enter_context(tc.psum_pool(name="sum_banks", bufs=4))
+        ctx.enter_context(tc.manual_schedule())
 
-        ident = const.tile([P, P], F32, name="ident")
-        sva = const.tile([P, 256], BF16, name="sva")
-        svb = const.tile([P, 256], BF16, name="svb")
-        v2g = const.tile([P, 32], F32, name="v2g")
-        cols = const.tile([P, 112], F32, name="cols")
-        cs = const.tile([P, 8], F32, name="cs")
+        identity = const.tile([P, P], F32, name="identity")
+        make_identity(nc, identity[:])
 
-        nc.vector.memset(sva[:].bitcast(F32), 0.0)
-        nc.vector.memset(svb[:].bitcast(F32), 0.0)
-        make_identity(nc, ident[:])
+        early_rows = const.tile([P, 256], BF16, name="early_rows")
+        late_rows = const.tile([P, 256], BF16, name="late_rows")
+        nc.vector.memset(early_rows[:].bitcast(F32), 0.0)
+        nc.vector.memset(late_rows[:].bitcast(F32), 0.0)
+        v2_words = const.tile([P, 32], F32, name="v2_words")
+        late_cols = const.tile([P, 112], F32, name="late_cols")
+        rank_scale = const.tile([P, 8], F32, name="rank_scale")
 
         def rows_of(vec):
             return vec.rearrange("o (r c) -> (o r) c", c=256)
 
-        nc.sync.dma_start(out=sva[0:16, :], in_=rows_of(v2))
-        nc.sync.dma_start(out=sva[16:32, :], in_=rows_of(v2_R))
+        nc.sync.dma_start(out=early_rows[0:16, :], in_=rows_of(v2))
+        nc.sync.dma_start(out=early_rows[16:32, :], in_=rows_of(v2_R))
 
-        order = []
+        load_order = []
         for c in range(8):
-            order.extend([("x", 0, c), ("v", 0, c)])
-        order.extend([("v", 1, c) for c in range(8)])
-        for grp in range(8):
-            order.extend([("u", 0, grp), ("u", 1, grp)])
+            load_order.extend([("x", 0, c), ("v", 0, c)])
+        load_order.extend([("v", 1, c) for c in range(8)])
+        for group in range(8):
+            load_order.extend([("u", 0, group), ("u", 1, group)])
         raw = {}
 
         def load_next():
-            if len(raw) == len(order):
+            if len(raw) == len(load_order):
                 return
-            kind, b, j = order[len(raw)]
-            t = rawp.tile([P, 2048], BF16, name="raw")
-            raw[(kind, b, j)] = t
-            t3 = t[:].rearrange("p (r k) -> p r k", r=4)
-            if kind == "x":
-                nc.sync.dma_start(out=t3, in_=x_view[:, :, 512 * j : 512 * (j + 1)])
-            elif kind == "v":
-                for u in range(2):
-                    nc.sync.dma_start(out=t3[:, 2 * u : 2 * u + 2, :], in_=v_views[b][u][:, :, 512 * j : 512 * (j + 1)])
-            else:
-                nc.sync.dma_start(out=t[:].rearrange("p (a k) -> p a k", a=2), in_=u_views[b][:, 2 * j : 2 * j + 2, :])
+            kind, b, j = load_order[len(raw)]
+            tile = raw_pool.tile([P, 2048], BF16, name="raw")
+            raw[(kind, b, j)] = tile
+            groups = tile[:].rearrange("p (r k) -> p r k", r=4)
+            if kind == "u":
+                nc.sync.dma_start(out=tile[:].rearrange("p (a k) -> p a k", a=2), in_=u_views[b][:, 2 * j : 2 * j + 2, :])
+                return
+            for a in range(2):
+                src = x_view[:, 2 * a : 2 * a + 2, :] if kind == "x" else v_views[b][a]
+                nc.sync.dma_start(out=groups[:, 2 * a : 2 * a + 2, :], in_=src[:, :, 512 * j : 512 * (j + 1)])
 
-        for first in range(RAW_BUFS):
+        for tile_no in range(RAW_TILES):
             load_next()
-        nc.sync.dma_start(out=svb[0:16, :], in_=rows_of(u1))
-        nc.sync.dma_start(out=svb[16:32, :], in_=rows_of(u1_R))
-        nc.sync.dma_start(out=svb[32:48, :], in_=bias.rearrange("(r c) -> r c", c=256))
-        nc.sync.dma_start(out=svb[48:50, :], in_=rows_of(v1))
-        nc.sync.dma_start(out=svb[50:52, :], in_=rows_of(u2))
-        nc.sync.dma_start(out=svb[52:54, :], in_=rows_of(v1_R))
-        nc.sync.dma_start(out=svb[54:56, :], in_=rows_of(u2_R))
-
-        def w_key(j):
-            return ("v", j // 8, j % 8) if j < 16 else ("u", j % 2, (j - 16) // 2)
-
-        def u_bank(s):
-            return (16 + 2 * (s // 4) + s % 2, (s % 4) // 2)
+        nc.sync.dma_start(out=late_rows[0:16, :], in_=rows_of(u1))
+        nc.sync.dma_start(out=late_rows[16:32, :], in_=rows_of(u1_R))
+        nc.sync.dma_start(out=late_rows[32:48, :], in_=bias.rearrange("(r c) -> r c", c=256))
+        nc.sync.dma_start(out=late_rows[48:50, :], in_=rows_of(v1))
+        nc.sync.dma_start(out=late_rows[50:52, :], in_=rows_of(u2))
+        nc.sync.dma_start(out=late_rows[52:54, :], in_=rows_of(v1_R))
+        nc.sync.dma_start(out=late_rows[54:56, :], in_=rows_of(u2_R))
 
         bank = {}
-        xt = {}
-        xv = {}
-        wg = {}
-        xcode = {}
-        wcode = {}
-        acc = {}
-        gcode = {}
-        gp = {}
-        gg = {}
-        ya = {}
-        yb = {}
-        t1 = {}
-        res = {}
-        ot = {}
+        x_words = {}
+        x_scaled = {}
+        signs = {}
+        x_codes = {}
+        w_codes = {}
+        u_codes = {}
+        g_codes = {}
+        h_sum = {}
+        g_planes = {}
+        g_grouped = {}
+        y_main = {}
+        y_residual = {}
+        scaled = {}
+        result = {}
+        turned = {}
 
-        def fill(key, h, pool, name):
-            b = pool.tile([P, 512], F32, name=name)
-            bank[(key, h)] = b
+        def transpose_half(key, half, pool, name):
+            bank[(key, half)] = pool.tile([P, 512], F32, name=name)
             words = raw[key][:].bitcast(F32)
             for u in range(2):
-                for j in range(2):
-                    col = (2 * h + j) * 256 + u * P
-                    nc.tensor.transpose(out=b[:, u * 256 + j * P : u * 256 + (j + 1) * P], in_=words[:, col : col + P], identity=ident[:])
-            if h == 1:
+                for r in range(2):
+                    col = (2 * half + r) * 256 + u * P
+                    nc.tensor.transpose(
+                        out=bank[(key, half)][:, u * 256 + r * P : u * 256 + (r + 1) * P],
+                        in_=words[:, col : col + P],
+                        identity=identity[:],
+                    )
+            if half == 1:
                 load_next()
 
-        def fill_u(s):
-            if s < 32:
-                fill(w_key(u_bank(s)[0]), u_bank(s)[1], wp, "wp")
+        def by_word(bank_tile):
+            return bank_tile[:].bitcast(BF16).rearrange("p (u c e) -> p c u e", u=2, e=2)
 
-        def sign_u(s):
-            j, h = u_bank(s)
-            wg[(j, h)] = four.tile([P, 1024], BF16, name="ug", align_bytes=64)
-            nc.scalar.activation(
-                out=wg[(j, h)][:].rearrange("p (c u e) -> p c u e", u=2, e=2),
-                in_=bank[(w_key(j), h)][:].bitcast(BF16).rearrange("p (u c e) -> p c u e", u=2, e=2),
-                func=ACT.Sign,
-            )
+        def as_words(ap):
+            return ap.rearrange("p (c u e) -> p c u e", u=2, e=2)
 
-        def quant_u(s):
-            if 0 <= s < 32:
-                codes = sixteen.tile([P, 256], U32, name="uc", align_bytes=64)
-                scales = sixteen.tile([P, 256], U8, name="us", align_bytes=64)
-                nc.vector.quantize_mx(out=codes[:].bitcast(FP8X4), scales=scales[:], in_=wg[u_bank(s)][:])
-                wcode[u_bank(s)] = (codes, scales)
-
-        def fill_w(j, h):
-            if j < 16:
-                fill(w_key(j), h, wp, "wp")
-            elif j == 16:
-                fill_u(0)
-
-        def fill_x(c, h):
-            if c < 8:
-                fill(("x", 0, c), h, xo, "xo")
-
-        def x_exit(c, h):
-            if h == 0:
-                xt[c] = eight.tile([P, 1024], F32, name="xt")
-            dst = xt[c][:, h * 512 : (h + 1) * 512].rearrange("p (n u) -> p n u", u=2)
-            src = bank[(("x", 0, c), h)][:].rearrange("p (u n) -> p n u", u=2)
-            if h == 0:
-                nc.scalar.copy(out=dst, in_=src)
-            else:
-                nc.vector.tensor_copy(out=dst, in_=src)
-
-        def sign(j, h):
-            if h == 0:
-                wg[j] = three.tile([P, 2048], BF16, name="wg", align_bytes=64)
-            nc.scalar.activation(
-                out=wg[j][:, h * 1024 : (h + 1) * 1024].rearrange("p (c u e) -> p c u e", u=2, e=2),
-                in_=bank[(w_key(j), h)][:].bitcast(BF16).rearrange("p (u c e) -> p c u e", u=2, e=2),
-                func=ACT.Sign,
-            )
-
-        def quantise(src, pool, name):
-            codes = pool.tile([P, 512], U32, name=name + "c", align_bytes=64)
-            scales = pool.tile([P, 512], U8, name=name + "s", align_bytes=64)
+        def quantise(src, width, pool, name):
+            codes = pool.tile([P, width], U32, name=name + "_codes", align_bytes=64)
+            scales = pool.tile([P, width], U8, name=name + "_scales", align_bytes=64)
             nc.vector.quantize_mx(out=codes[:].bitcast(FP8X4), scales=scales[:], in_=src[:])
             return (codes, scales)
 
-        def quant_w(j):
-            if 0 <= j < 16:
-                wcode[j] = quantise(wg[j], four, "w")
-
-        def mul_x(j):
-            if j < 16:
-                b, c = j // 8, j % 8
-                xv[j] = three.tile([P, 2048], BF16, name="xv", align_bytes=64)
-                nc.vector.tensor_tensor(
-                    out=xv[j][:].rearrange("p (n t) -> p n t", t=4),
-                    in0=xt[c][:].bitcast(BF16).rearrange("p (n t) -> p n t", t=4),
-                    in1=v2g[:].bitcast(BF16)[:, 32 * b + 4 * c : 32 * b + 4 * c + 4].unsqueeze(1).to_broadcast([P, 512, 4]),
-                    op=ALU.mult,
-                )
-
-        def quant_x(j):
-            if 0 <= j < 16:
-                xcode[j] = quantise(xv[j], four, "x")
-
-        def mx(dst, lhs, t, rhs, start, stop):
+        def mx_pass(dst, weights, col, moving, start, stop):
             nc.tensor.matmul_mx(
                 out=dst[:],
-                lhsT=lhs[0][:, t * P : (t + 1) * P].bitcast(FP8X4),
-                lhsT_scale=lhs[1][:, t * P : (t + 1) * P],
-                rhs=rhs[0][:].bitcast(FP8X4),
-                rhs_scale=rhs[1][:],
+                lhsT=weights[0][:, col * P : (col + 1) * P].bitcast(FP8X4),
+                lhsT_scale=weights[1][:, col * P : (col + 1) * P],
+                rhs=moving[0][:].bitcast(FP8X4),
+                rhs_scale=moving[1][:],
                 start=start,
                 stop=stop,
             )
 
-        def stage1(j):
-            if 0 <= j < 16:
+        def transpose_x(c, half):
+            if c < 8:
+                transpose_half(("x", 0, c), half, turn_banks, "turn")
+
+        def transpose_v(j, half):
+            if j < STEPS:
+                transpose_half(("v", j // 8, j % 8), half, weight_banks, "weights")
+
+        def keep_x(c, half):
+            if half == 0:
+                x_words[c] = eight.tile([P, 1024], F32, name="x_words")
+            dst = x_words[c][:, half * 512 : (half + 1) * 512].rearrange("p (n u) -> p n u", u=2)
+            src = bank[(("x", 0, c), half)][:].rearrange("p (u n) -> p n u", u=2)
+            if half == 0:
+                nc.scalar.copy(out=dst, in_=src)
+            else:
+                nc.vector.tensor_copy(out=dst, in_=src)
+
+        def scale_x(j):
+            if j < STEPS:
                 b, c = j // 8, j % 8
-                for t in range(4):
-                    if c == 0:
-                        acc[(b, t)] = accp.tile([P, 512], F32, name="acc")
-                    mx(acc[(b, t)], wcode[j], t, xcode[j], c == 0, c == 7)
-
-        def h_exit(b, engine):
-            if b not in gp:
-                gp[b] = const.tile([P, 4, 512], BF16, name="gp%d" % b)
-            for t in range(4):
-                scale = cs[:, 4 * b + t : 4 * b + t + 1]
-                if t % 2 == 0 and engine == "s":
-                    nc.scalar.activation(out=gp[b][:, t, :], in_=acc[(b, t)][:], func=ACT.Copy, scale=scale)
-                if t % 2 == 1 and engine == "v":
-                    nc.vector.tensor_scalar(out=gp[b][:, t, :], in0=acc[(b, t)][:], scalar1=scale, scalar2=None, op0=ALU.mult)
-
-        def regroup_g(b):
-            gg[b] = const.tile([P, 2048], BF16, name="gg%d" % b, align_bytes=64)
-            nc.vector.tensor_copy(out=gg[b][:].rearrange("p (n t) -> p n t", t=4), in_=gp[b][:].rearrange("p t n -> p n t"))
-
-        def quant_g(b):
-            gcode[b] = quantise(gg[b], const, "g%d" % b)
-
-        def stage2(q, b):
-            if 0 <= q < 32:
-                y = accp.tile([P, 512], F32, name="acc")
-                (ya if b == 0 else yb)[q] = y
-                mx(y, wcode[(16 + 2 * (q // 4) + b, (q % 4) // 2)], q % 2, gcode[b], True, True)
-
-        def scale_main(q, engine):
-            if 0 <= q < 32 and (engine == "v") == (q % 4 == V_E1):
-                t1[q] = three.tile([P, 512], F32, name="t1")
-                if engine == "v":
-                    nc.vector.tensor_scalar(
-                        out=t1[q][:], in0=ya[q][:], scalar1=cols[:, q : q + 1], scalar2=cols[:, 64 + q : 65 + q], op0=ALU.mult, op1=ALU.add
-                    )
-                else:
-                    nc.scalar.activation(
-                        out=t1[q][:], in_=ya[q][:], func=ACT.Identity, scale=cols[:, q : q + 1], bias=cols[:, 64 + q : 65 + q]
-                    )
-
-        def add_residual(q):
-            if 0 <= q < 32:
-                res[q] = eight.tile([P, 512], F32, name="res")
-                nc.vector.scalar_tensor_tensor(
-                    out=res[q][:], in0=yb[q][:], scalar=cols[:, 32 + q : 33 + q], in1=t1[q][:], op0=ALU.mult, op1=ALU.add
+                x_scaled[j] = three.tile([P, 2048], BF16, name="x_scaled", align_bytes=64)
+                v2_of_word = v2_words[:].bitcast(BF16)[:, 32 * b + 4 * c : 32 * b + 4 * c + 4]
+                nc.vector.tensor_tensor(
+                    out=x_scaled[j][:].rearrange("p (n t) -> p n t", t=4),
+                    in0=x_words[c][:].bitcast(BF16).rearrange("p (n t) -> p n t", t=4),
+                    in1=v2_of_word.unsqueeze(1).to_broadcast([P, 512, 4]),
+                    op=ALU.mult,
                 )
 
-        def back(q):
-            if 0 <= q < 32:
-                grp, i = q // 4, q % 4
-                ot[q] = xo.tile([P, 512], F32, name="xo")
-                for t in range(4):
-                    nc.tensor.transpose(
-                        out=ot[q][:, t * P : (t + 1) * P], in_=res[4 * grp + t][:, i * P : (i + 1) * P], identity=ident[:]
-                    )
+        def quantise_x(j):
+            if 0 <= j < STEPS:
+                x_codes[j] = quantise(x_scaled[j], 512, four, "x")
+
+        def sign_v(j, half):
+            if half == 0:
+                signs[j] = three.tile([P, 2048], BF16, name="v_signs", align_bytes=64)
+            nc.scalar.activation(
+                out=as_words(signs[j][:, half * 1024 : (half + 1) * 1024]),
+                in_=by_word(bank[(("v", j // 8, j % 8), half)]),
+                func=ACT.Sign,
+            )
+
+        def quantise_v(j):
+            if 0 <= j < STEPS:
+                w_codes[j] = quantise(signs[j], 512, four, "v")
+
+        def stage1_passes(j):
+            if 0 <= j < STEPS:
+                b, c = j // 8, j % 8
+                for r in range(4):
+                    if c == 0:
+                        h_sum[(b, r)] = sum_banks.tile([P, 512], F32, name="sums")
+                    mx_pass(h_sum[(b, r)], w_codes[j], r, x_codes[j], c == 0, c == 7)
+
+        def scale_h(b):
+            g_planes[b] = const.tile([P, 4, 512], BF16, name="g_planes%d" % b)
+            for r in (0, 2):
+                nc.scalar.activation(
+                    out=g_planes[b][:, r, :], in_=h_sum[(b, r)][:], func=ACT.Copy, scale=rank_scale[:, 4 * b + r : 4 * b + r + 1]
+                )
+            for r in (1, 3):
+                nc.vector.tensor_scalar(
+                    out=g_planes[b][:, r, :],
+                    in0=h_sum[(b, r)][:],
+                    scalar1=rank_scale[:, 4 * b + r : 4 * b + r + 1],
+                    scalar2=None,
+                    op0=ALU.mult,
+                )
+
+        def group_g(b):
+            g_grouped[b] = const.tile([P, 2048], BF16, name="g_grouped%d" % b, align_bytes=64)
+            nc.vector.tensor_copy(
+                out=g_grouped[b][:].rearrange("p (n t) -> p n t", t=4), in_=g_planes[b][:].rearrange("p t n -> p n t")
+            )
+
+        def quantise_g(b):
+            g_codes[b] = quantise(g_grouped[b], 512, const, "g%d" % b)
+
+        def u_bank(s):
+            return (("u", s % 2, s // 4), (s % 4) // 2)
+
+        def transpose_u(s):
+            if s < TILES:
+                transpose_half(u_bank(s)[0], u_bank(s)[1], weight_banks, "weights")
+
+        def sign_u(s):
+            if s < TILES:
+                signs[u_bank(s)] = four.tile([P, 1024], BF16, name="u_signs", align_bytes=64)
+                nc.scalar.activation(out=as_words(signs[u_bank(s)][:]), in_=by_word(bank[u_bank(s)]), func=ACT.Sign)
+
+        def quantise_u(s):
+            if 0 <= s < TILES:
+                u_codes[u_bank(s)] = quantise(signs[u_bank(s)], 256, sixteen, "u")
+
+        def stage2_pass(q, b):
+            if 0 <= q < TILES:
+                sums = sum_banks.tile([P, 512], F32, name="sums")
+                (y_main if b == 0 else y_residual)[q] = sums
+                mx_pass(sums, u_codes[(("u", b, q // 4), (q % 4) // 2)], q % 2, g_codes[b], True, True)
+
+        def on_vector(q):
+            return q % 4 == 3
+
+        def scale_main(q):
+            scaled[q] = three.tile([P, 512], F32, name="scaled")
+            u1_col, bias_col = late_cols[:, q : q + 1], late_cols[:, 64 + q : 65 + q]
+            if on_vector(q):
+                nc.vector.tensor_scalar(out=scaled[q][:], in0=y_main[q][:], scalar1=u1_col, scalar2=bias_col, op0=ALU.mult, op1=ALU.add)
+            else:
+                nc.scalar.activation(out=scaled[q][:], in_=y_main[q][:], func=ACT.Identity, scale=u1_col, bias=bias_col)
+
+        def add_residual(q):
+            if 0 <= q < TILES:
+                result[q] = eight.tile([P, 512], F32, name="result")
+                nc.vector.scalar_tensor_tensor(
+                    out=result[q][:],
+                    in0=y_residual[q][:],
+                    scalar=late_cols[:, 32 + q : 33 + q],
+                    in1=scaled[q][:],
+                    op0=ALU.mult,
+                    op1=ALU.add,
+                )
+
+        def turn_back(q):
+            if 0 <= q < TILES:
+                turned[q] = turn_banks.tile([P, 512], F32, name="turn")
+                for i in range(2):
+                    for e in range(2):
+                        tokens = (2 * (q % 2) + i) * P
+                        nc.tensor.transpose(
+                            out=turned[q][:, (2 * i + e) * P : (2 * i + e + 1) * P],
+                            in_=result[2 * (q // 2) + e][:, tokens : tokens + P],
+                            identity=identity[:],
+                        )
 
         def store(q, engine):
-            if 0 <= q < 32:
-                grp, i = q // 4, q % 4
-                ob = four.tile([P, 512], F32, name="ob")
-                dst = ob[:].rearrange("p (h m e) -> p h m e", h=2, e=2)
-                src = ot[q][:].rearrange("p (h e m) -> p h m e", h=2, e=2)
-                if engine == "s":
+            if 0 <= q < TILES:
+                rows = four.tile([P, 512], F32, name="rows")
+                dst = rows[:].rearrange("p (i m e) -> p i m e", i=2, e=2)
+                src = turned[q][:].rearrange("p (i e m) -> p i m e", i=2, e=2)
+                if engine == "scalar":
                     nc.scalar.copy(out=dst, in_=src)
                 else:
                     nc.vector.tensor_copy(out=dst, in_=src)
-                nc.sync.dma_start(out=out_rows[i * P : (i + 1) * P, grp * 512 : (grp + 1) * 512], in_=ob[:])
+                nc.sync.dma_start(
+                    out=out_view[:, 2 * (q % 2) : 2 * (q % 2) + 2, (q // 2) * 256 : (q // 2 + 1) * 256],
+                    in_=rows[:].rearrange("p (i o) -> p i o", i=2),
+                )
 
-        spread_a = xo.tile([P, 512], F32, name="xo")
-        nc.tensor.transpose(out=spread_a[:, 0:P], in_=sva[:].bitcast(F32), identity=ident[:])
-        nc.vector.tensor_copy(out=v2g[:], in_=spread_a[:, 0:32])
+        early_cols = turn_banks.tile([P, 512], F32, name="turn")
+        nc.tensor.transpose(out=early_cols[:, 0:P], in_=early_rows[:].bitcast(F32), identity=identity[:])
+        nc.vector.tensor_copy(out=v2_words[:], in_=early_cols[:, 0:32])
 
-        fill_x(0, 0)
-        fill_x(0, 1)
-        fill_w(0, 0)
-        for j in range(16):
-            fill_w(j, 1)
-            stage1(j - 2)
+        transpose_x(0, 0)
+        transpose_x(0, 1)
+        transpose_v(0, 0)
+        for j in range(STEPS):
+            transpose_v(j, 1)
+            stage1_passes(j - 2)
             if j < 8:
-                x_exit(j, 0)
-                x_exit(j, 1)
-                fill_x(j + 1, 0)
-                fill_x(j + 1, 1)
+                keep_x(j, 0)
+                keep_x(j, 1)
+                transpose_x(j + 1, 0)
+                transpose_x(j + 1, 1)
             if j == 8:
-                spread_b = xo.tile([P, 512], F32, name="xo")
-                nc.tensor.transpose(out=spread_b[:, 0:P], in_=svb[:].bitcast(F32), identity=ident[:])
+                late_bank = turn_banks.tile([P, 512], F32, name="turn")
+                nc.tensor.transpose(out=late_bank[:, 0:P], in_=late_rows[:].bitcast(F32), identity=identity[:])
             if j == 9:
-                nc.vector.tensor_copy(out=cols[:], in_=spread_b[:, 0:56].bitcast(BF16))
+                nc.vector.tensor_copy(out=late_cols[:], in_=late_bank[:, 0:56].bitcast(BF16))
                 for b in range(2):
                     nc.vector.tensor_tensor(
-                        out=cs[:, 4 * b : 4 * b + 4],
-                        in0=cols[:, 96 + 8 * b : 100 + 8 * b],
-                        in1=cols[:, 100 + 8 * b : 104 + 8 * b],
+                        out=rank_scale[:, 4 * b : 4 * b + 4],
+                        in0=late_cols[:, 96 + 8 * b : 100 + 8 * b],
+                        in1=late_cols[:, 100 + 8 * b : 104 + 8 * b],
                         op=ALU.mult,
                     )
-            quant_x(j - 1)
-            mul_x(j)
-            sign(j, 0)
-            fill_w(j + 1, 0)
-            sign(j, 1)
-            quant_w(j - 1)
+            quantise_x(j - 1)
+            scale_x(j)
+            sign_v(j, 0)
+            if j + 1 < STEPS:
+                transpose_v(j + 1, 0)
+            else:
+                transpose_u(0)
+            sign_v(j, 1)
+            quantise_v(j - 1)
             if j == 9:
-                h_exit(0, "s")
-                h_exit(0, "v")
+                scale_h(0)
 
-        for s in range(32 + D3 + 4):
+        for s in range(LAST_SLOT + 1):
             if s == 0:
-                quant_x(15)
-                quant_w(15)
-            quant_u(s - 1)
-            fill_u(s + 1)
-            back(s - DO)
+                quantise_x(STEPS - 1)
+                quantise_v(STEPS - 1)
+            quantise_u(s - 1)
+            transpose_u(s + 1)
+            turn_back(s - BACK)
             if s == 0:
-                stage1(14)
+                stage1_passes(STEPS - 2)
             if s == 1:
-                stage1(15)
-                regroup_g(0)
-                quant_g(0)
-            stage2(s - DB, 1)
-            stage2(s - DA, 0)
-            if s < 32:
-                sign_u(s)
+                stage1_passes(STEPS - 1)
+                group_g(0)
+            stage2_pass(s - RESIDUAL_PASS, 1)
+            stage2_pass(s - MAIN_PASS, 0)
+            sign_u(s)
             if s == 2:
-                h_exit(1, "s")
-                h_exit(1, "v")
+                quantise_g(0)
+                scale_h(1)
             if s == 3:
-                regroup_g(1)
+                group_g(1)
             if s == 4:
-                quant_g(1)
-            scale_main(s - D1, "s")
-            store(s - D3, "s" if s >= S_E3_FROM else "v")
-            add_residual(s - D2)
-            scale_main(s - D1, "v")
+                quantise_g(1)
+            q = s - SCALE
+            if 0 <= q < TILES and not on_vector(q):
+                scale_main(q)
+            store(s - STORE, "scalar" if s > TILES else "vector")
+            add_residual(s - ADD)
+            if 0 <= q < TILES and on_vector(q):
+                scale_main(q)

@@ -14,17 +14,14 @@ ALU = mybir.AluOpType
 FLOPS = 2 * 2 * 2 * 512 * 4096 * 512
 
 P = 128
-STEPS = 16
+PASSES = 8
 TILES = 32
-RAW_TILES = 16
+RAW_TILES = 8
+RAW_U_TILES = 6
 
-MAIN_PASS = 4
-RESIDUAL_PASS = 5
-SCALE = 5
-ADD = 6
-BACK = 8
-STORE = 9
-LAST_SLOT = TILES - 1 + STORE
+PAIRS = TILES // 2
+
+TINY = 2.0 ** -119
 
 
 def tile_littlebitlinear_pa_kernel(
@@ -39,10 +36,13 @@ def tile_littlebitlinear_pa_kernel(
     with ExitStack() as ctx:
         const = ctx.enter_context(tc.tile_pool(name="const", bufs=1))
         raw_pool = ctx.enter_context(tc.tile_pool(name="raw_pool", bufs=RAW_TILES))
+        raw_u_pool = ctx.enter_context(tc.tile_pool(name="raw_u_pool", bufs=RAW_U_TILES))
+        two = ctx.enter_context(tc.tile_pool(name="two", bufs=2))
         three = ctx.enter_context(tc.tile_pool(name="three", bufs=3))
         four = ctx.enter_context(tc.tile_pool(name="four", bufs=4))
+        six = ctx.enter_context(tc.tile_pool(name="six", bufs=6))
         eight = ctx.enter_context(tc.tile_pool(name="eight", bufs=8))
-        sixteen = ctx.enter_context(tc.tile_pool(name="sixteen", bufs=16))
+        twenty = ctx.enter_context(tc.tile_pool(name="twenty", bufs=20))
         weight_banks = ctx.enter_context(tc.psum_pool(name="weight_banks", bufs=2))
         turn_banks = ctx.enter_context(tc.psum_pool(name="turn_banks", bufs=2))
         sum_banks = ctx.enter_context(tc.psum_pool(name="sum_banks", bufs=4))
@@ -55,6 +55,11 @@ def tile_littlebitlinear_pa_kernel(
         late_rows = const.tile([P, 256], BF16, name="late_rows")
         nc.vector.memset(early_rows[:].bitcast(F32), 0.0)
         nc.vector.memset(late_rows[:].bitcast(F32), 0.0)
+        ones = const.tile([P, 512], BF16, name="ones", align_bytes=64)
+        nc.vector.memset(ones[:], 1.0)
+        ones_codes = const.tile([P, P], U32, name="ones_codes", align_bytes=64)
+        ones_scales = const.tile([P, P], U8, name="ones_scales", align_bytes=64)
+        nc.vector.quantize_mx(out=ones_codes[:].bitcast(FP8X4), scales=ones_scales[:], in_=ones[:])
         v2_words = const.tile([P, 32], F32, name="v2_words")
         late_cols = const.tile([P, 112], F32, name="late_cols")
         rank_scale = const.tile([P, 8], F32, name="rank_scale")
@@ -65,40 +70,40 @@ def tile_littlebitlinear_pa_kernel(
         nc.sync.dma_start(out=early_rows[0:16, :], in_=rows_of(v2))
         nc.sync.dma_start(out=early_rows[16:32, :], in_=rows_of(v2_R))
 
-        load_order = []
-        for c in range(8):
-            load_order.extend([("x", 0, c), ("v", 0, c)])
-        load_order.extend([("v", 1, c) for c in range(8)])
-        for group in range(8):
-            load_order.extend([("u", 0, group), ("u", 1, group)])
         raw = {}
+        load_order = [(kind, b, c) for c in range(PASSES) for kind, b in (("x", 0), ("v", 0), ("v", 1))]
+        u_load_order = [("u", b, group) for group in range(8) for b in range(2)]
 
         def load_next():
-            if len(raw) == len(load_order):
-                return
-            kind, b, j = load_order[len(raw)]
-            tile = raw_pool.tile([P, 2048], BF16, name="raw")
-            raw[(kind, b, j)] = tile
-            groups = tile[:].rearrange("p (r k) -> p r k", r=4)
-            if kind == "u":
-                nc.sync.dma_start(out=tile[:].rearrange("p (a k) -> p a k", a=2), in_=u_views[b][:, 2 * j : 2 * j + 2, :])
-                return
-            for a in range(2):
-                src = x_view[:, 2 * a : 2 * a + 2, :] if kind == "x" else v_views[b][a]
-                nc.sync.dma_start(out=groups[:, 2 * a : 2 * a + 2, :], in_=src[:, :, 512 * j : 512 * (j + 1)])
+            if load_order:
+                kind, b, c = key = load_order.pop(0)
+                raw[key] = raw_pool.tile([P, 2048], BF16, name="raw")
+                groups = raw[key][:].rearrange("p (r k) -> p r k", r=4)
+                for a in range(2):
+                    src = x_view[:, 2 * a : 2 * a + 2, :] if kind == "x" else v_views[b][a]
+                    nc.sync.dma_start(out=groups[:, 2 * a : 2 * a + 2, :], in_=src[:, :, 512 * c : 512 * (c + 1)])
+
+        def load_next_u():
+            if u_load_order:
+                kind, b, group = key = u_load_order.pop(0)
+                raw[key] = raw_u_pool.tile([P, 2048], BF16, name="raw_u")
+                nc.sync.dma_start(
+                    out=raw[key][:].rearrange("p (a k) -> p a k", a=2), in_=u_views[b][:, 2 * group : 2 * group + 2, :]
+                )
 
         for tile_no in range(RAW_TILES):
             load_next()
-        nc.sync.dma_start(out=late_rows[0:16, :], in_=rows_of(u1))
-        nc.sync.dma_start(out=late_rows[16:32, :], in_=rows_of(u1_R))
-        nc.sync.dma_start(out=late_rows[32:48, :], in_=bias.rearrange("(r c) -> r c", c=256))
-        nc.sync.dma_start(out=late_rows[48:50, :], in_=rows_of(v1))
-        nc.sync.dma_start(out=late_rows[50:52, :], in_=rows_of(u2))
-        nc.sync.dma_start(out=late_rows[52:54, :], in_=rows_of(v1_R))
-        nc.sync.dma_start(out=late_rows[54:56, :], in_=rows_of(u2_R))
+
+        def load_late_rows():
+            nc.sync.dma_start(out=late_rows[0:16, :], in_=rows_of(u1))
+            nc.sync.dma_start(out=late_rows[16:32, :], in_=rows_of(u1_R))
+            nc.sync.dma_start(out=late_rows[32:48, :], in_=bias.rearrange("(r c) -> r c", c=256))
+            nc.sync.dma_start(out=late_rows[48:50, :], in_=rows_of(v1))
+            nc.sync.dma_start(out=late_rows[50:52, :], in_=rows_of(u2))
+            nc.sync.dma_start(out=late_rows[52:54, :], in_=rows_of(v1_R))
+            nc.sync.dma_start(out=late_rows[54:56, :], in_=rows_of(u2_R))
 
         bank = {}
-        x_words = {}
         x_scaled = {}
         signs = {}
         x_codes = {}
@@ -126,7 +131,7 @@ def tile_littlebitlinear_pa_kernel(
                         identity=identity[:],
                     )
             if half == 1:
-                load_next()
+                (load_next_u if key[0] == "u" else load_next)()
 
         def by_word(bank_tile):
             return bank_tile[:].bitcast(BF16).rearrange("p (u c e) -> p c u e", u=2, e=2)
@@ -140,92 +145,84 @@ def tile_littlebitlinear_pa_kernel(
             nc.vector.quantize_mx(out=codes[:].bitcast(FP8X4), scales=scales[:], in_=src[:])
             return (codes, scales)
 
+        def quantise_signs(src, width, pool, name):
+            codes = pool.tile([P, width], U32, name=name + "_codes", align_bytes=64)
+            unused = two.tile([P, 512], U8, name="unused", align_bytes=64)
+            nc.vector.quantize_mx(out=codes[:].bitcast(FP8X4), scales=unused[:, 0:width], in_=src[:])
+            return codes
+
         def mx_pass(dst, weights, col, moving, start, stop):
             nc.tensor.matmul_mx(
                 out=dst[:],
-                lhsT=weights[0][:, col * P : (col + 1) * P].bitcast(FP8X4),
-                lhsT_scale=weights[1][:, col * P : (col + 1) * P],
+                lhsT=weights[:, col * P : (col + 1) * P].bitcast(FP8X4),
+                lhsT_scale=ones_scales[:],
                 rhs=moving[0][:].bitcast(FP8X4),
                 rhs_scale=moving[1][:],
                 start=start,
                 stop=stop,
             )
 
+        def take_signs(dst, bank_tile, engine):
+            if engine == "scalar":
+                nc.scalar.activation(out=as_words(dst), in_=by_word(bank_tile), func=ACT.Sign)
+            else:
+                nc.vector.tensor_scalar(
+                    out=as_words(dst), in0=by_word(bank_tile), scalar1=-TINY, scalar2=TINY, op0=ALU.max, op1=ALU.min
+                )
+
         def transpose_x(c, half):
-            if c < 8:
+            if c < PASSES:
                 transpose_half(("x", 0, c), half, turn_banks, "turn")
 
-        def transpose_v(j, half):
-            if j < STEPS:
-                transpose_half(("v", j // 8, j % 8), half, weight_banks, "weights")
+        def transpose_v(b, c, half):
+            if c < PASSES:
+                transpose_half(("v", b, c), half, weight_banks, "weights")
 
-        def keep_x(c, half):
-            if half == 0:
-                x_words[c] = eight.tile([P, 1024], F32, name="x_words")
-            dst = x_words[c][:, half * 512 : (half + 1) * 512].rearrange("p (n u) -> p n u", u=2)
-            src = bank[(("x", 0, c), half)][:].rearrange("p (u n) -> p n u", u=2)
-            if half == 0:
-                nc.scalar.copy(out=dst, in_=src)
-            else:
-                nc.vector.tensor_copy(out=dst, in_=src)
-
-        def scale_x(j):
-            if j < STEPS:
-                b, c = j // 8, j % 8
-                x_scaled[j] = three.tile([P, 2048], BF16, name="x_scaled", align_bytes=64)
+        def scale_x(c, half):
+            for b in range(2):
+                if half == 0:
+                    x_scaled[(b, c)] = (two, eight)[b].tile([P, 2048], BF16, name="x_scaled%d" % b, align_bytes=64)
                 v2_of_word = v2_words[:].bitcast(BF16)[:, 32 * b + 4 * c : 32 * b + 4 * c + 4]
                 nc.vector.tensor_tensor(
-                    out=x_scaled[j][:].rearrange("p (n t) -> p n t", t=4),
-                    in0=x_words[c][:].bitcast(BF16).rearrange("p (n t) -> p n t", t=4),
-                    in1=v2_of_word.unsqueeze(1).to_broadcast([P, 512, 4]),
+                    out=as_words(x_scaled[(b, c)][:, half * 1024 : (half + 1) * 1024]),
+                    in0=by_word(bank[(("x", 0, c), half)]),
+                    in1=v2_of_word.rearrange("p (u e) -> p u e", u=2).unsqueeze(1).to_broadcast([P, 256, 2, 2]),
                     op=ALU.mult,
                 )
 
-        def quantise_x(j):
-            if 0 <= j < STEPS:
-                x_codes[j] = quantise(x_scaled[j], 512, four, "x")
-
-        def sign_v(j, half):
+        def sign_v(b, c, half, engine):
             if half == 0:
-                signs[j] = three.tile([P, 2048], BF16, name="v_signs", align_bytes=64)
-            nc.scalar.activation(
-                out=as_words(signs[j][:, half * 1024 : (half + 1) * 1024]),
-                in_=by_word(bank[(("v", j // 8, j % 8), half)]),
-                func=ACT.Sign,
-            )
+                signs[(b, c)] = (three, eight)[b].tile([P, 2048], BF16, name="v_signs%d" % b, align_bytes=64)
+            take_signs(signs[(b, c)][:, half * 1024 : (half + 1) * 1024], bank[(("v", b, c), half)], engine)
 
-        def quantise_v(j):
-            if 0 <= j < STEPS:
-                w_codes[j] = quantise(signs[j], 512, four, "v")
+        def quantise_stage1(b, c):
+            if 0 <= c < PASSES:
+                x_codes[(b, c)] = quantise(x_scaled[(b, c)], 512, three, "x")
+                w_codes[(b, c)] = quantise_signs(signs[(b, c)], 512, three, "v")
 
-        def stage1_passes(j):
-            if 0 <= j < STEPS:
-                b, c = j // 8, j % 8
-                for r in range(4):
-                    if c == 0:
-                        h_sum[(b, r)] = sum_banks.tile([P, 512], F32, name="sums")
-                    mx_pass(h_sum[(b, r)], w_codes[j], r, x_codes[j], c == 0, c == 7)
+        def stage1_pass(b, c, r):
+            if 0 <= c < PASSES:
+                if c == 0:
+                    h_sum[(b, r)] = sum_banks.tile([P, 512], F32, name="sums")
+                mx_pass(h_sum[(b, r)], w_codes[(b, c)], r, x_codes[(b, c)], c == 0, c == PASSES - 1)
 
-        def scale_h(b):
-            g_planes[b] = const.tile([P, 4, 512], BF16, name="g_planes%d" % b)
-            for r in (0, 2):
-                nc.scalar.activation(
-                    out=g_planes[b][:, r, :], in_=h_sum[(b, r)][:], func=ACT.Copy, scale=rank_scale[:, 4 * b + r : 4 * b + r + 1]
-                )
-            for r in (1, 3):
-                nc.vector.tensor_scalar(
-                    out=g_planes[b][:, r, :],
-                    in0=h_sum[(b, r)][:],
-                    scalar1=rank_scale[:, 4 * b + r : 4 * b + r + 1],
-                    scalar2=None,
-                    op0=ALU.mult,
-                )
+        def scale_h(b, r, engine):
+            if r == 0:
+                g_planes[b] = two.tile([P, 4, 512], BF16, name="x_scaled0", align_bytes=64)
+            column = rank_scale[:, 4 * b + r : 4 * b + r + 1]
+            if engine == "scalar":
+                nc.scalar.activation(out=g_planes[b][:, r, :], in_=h_sum[(b, r)][:], func=ACT.Copy, scale=column)
+            else:
+                nc.vector.tensor_scalar(out=g_planes[b][:, r, :], in0=h_sum[(b, r)][:], scalar1=column, scalar2=None, op0=ALU.mult)
 
-        def group_g(b):
-            g_grouped[b] = const.tile([P, 2048], BF16, name="g_grouped%d" % b, align_bytes=64)
-            nc.vector.tensor_copy(
-                out=g_grouped[b][:].rearrange("p (n t) -> p n t", t=4), in_=g_planes[b][:].rearrange("p t n -> p n t")
-            )
+        def group_g(b, engine):
+            g_grouped[b] = three.tile([P, 2048], BF16, name="v_signs0", align_bytes=64)
+            dst = g_grouped[b][:].rearrange("p (n t) -> p n t", t=4)
+            src = g_planes[b][:].rearrange("p t n -> p n t")
+            if engine == "scalar":
+                nc.scalar.copy(out=dst, in_=src)
+            else:
+                nc.vector.tensor_copy(out=dst, in_=src)
 
         def quantise_g(b):
             g_codes[b] = quantise(g_grouped[b], 512, const, "g%d" % b)
@@ -237,35 +234,35 @@ def tile_littlebitlinear_pa_kernel(
             if s < TILES:
                 transpose_half(u_bank(s)[0], u_bank(s)[1], weight_banks, "weights")
 
-        def sign_u(s):
+        def sign_u(s, engine):
             if s < TILES:
                 signs[u_bank(s)] = four.tile([P, 1024], BF16, name="u_signs", align_bytes=64)
-                nc.scalar.activation(out=as_words(signs[u_bank(s)][:]), in_=by_word(bank[u_bank(s)]), func=ACT.Sign)
+                take_signs(signs[u_bank(s)][:], bank[u_bank(s)], engine)
 
         def quantise_u(s):
             if 0 <= s < TILES:
-                u_codes[u_bank(s)] = quantise(signs[u_bank(s)], 256, sixteen, "u")
+                u_codes[u_bank(s)] = quantise_signs(signs[u_bank(s)], 256, twenty, "u")
 
         def stage2_pass(q, b):
-            if 0 <= q < TILES:
+            if q < TILES:
                 sums = sum_banks.tile([P, 512], F32, name="sums")
                 (y_main if b == 0 else y_residual)[q] = sums
                 mx_pass(sums, u_codes[(("u", b, q // 4), (q % 4) // 2)], q % 2, g_codes[b], True, True)
 
-        def on_vector(q):
-            return q % 4 == 3
-
         def scale_main(q):
-            scaled[q] = three.tile([P, 512], F32, name="scaled")
-            u1_col, bias_col = late_cols[:, q : q + 1], late_cols[:, 64 + q : 65 + q]
-            if on_vector(q):
-                nc.vector.tensor_scalar(out=scaled[q][:], in0=y_main[q][:], scalar1=u1_col, scalar2=bias_col, op0=ALU.mult, op1=ALU.add)
-            else:
-                nc.scalar.activation(out=scaled[q][:], in_=y_main[q][:], func=ACT.Identity, scale=u1_col, bias=bias_col)
+            if 0 <= q < TILES:
+                scaled[q] = three.tile([P, 512], F32, name="scaled")
+                nc.scalar.activation(
+                    out=scaled[q][:],
+                    in_=y_main[q][:],
+                    func=ACT.Identity,
+                    scale=late_cols[:, q : q + 1],
+                    bias=late_cols[:, 64 + q : 65 + q],
+                )
 
         def add_residual(q):
             if 0 <= q < TILES:
-                result[q] = eight.tile([P, 512], F32, name="result")
+                result[q] = six.tile([P, 512], F32, name="result")
                 nc.vector.scalar_tensor_tensor(
                     out=result[q][:],
                     in0=y_residual[q][:],
@@ -306,66 +303,97 @@ def tile_littlebitlinear_pa_kernel(
         nc.vector.tensor_copy(out=v2_words[:], in_=early_cols[:, 0:32])
 
         transpose_x(0, 0)
+        transpose_v(0, 0, 0)
         transpose_x(0, 1)
-        transpose_v(0, 0)
-        for j in range(STEPS):
-            transpose_v(j, 1)
-            stage1_passes(j - 2)
-            if j < 8:
-                keep_x(j, 0)
-                keep_x(j, 1)
-                transpose_x(j + 1, 0)
-                transpose_x(j + 1, 1)
-            if j == 8:
-                late_bank = turn_banks.tile([P, 512], F32, name="turn")
-                nc.tensor.transpose(out=late_bank[:, 0:P], in_=late_rows[:].bitcast(F32), identity=identity[:])
-            if j == 9:
-                nc.vector.tensor_copy(out=late_cols[:], in_=late_bank[:, 0:56].bitcast(BF16))
-                for b in range(2):
-                    nc.vector.tensor_tensor(
-                        out=rank_scale[:, 4 * b : 4 * b + 4],
-                        in0=late_cols[:, 96 + 8 * b : 100 + 8 * b],
-                        in1=late_cols[:, 100 + 8 * b : 104 + 8 * b],
-                        op=ALU.mult,
-                    )
-            quantise_x(j - 1)
-            scale_x(j)
-            sign_v(j, 0)
-            if j + 1 < STEPS:
-                transpose_v(j + 1, 0)
+        for c in range(PASSES):
+            transpose_v(0, c, 1)
+            for r in range(4):
+                stage1_pass(0, c - 2, r)
+            scale_x(c, 0)
+            sign_v(0, c, 0, "scalar")
+            transpose_v(1, c, 0)
+            transpose_x(c + 1, 0)
+            scale_x(c, 1)
+            sign_v(0, c, 1, "scalar")
+            transpose_v(1, c, 1)
+            transpose_x(c + 1, 1)
+            sign_v(1, c, 0, "scalar")
+            if c < PASSES - 1:
+                transpose_v(0, c + 1, 0)
             else:
                 transpose_u(0)
-            sign_v(j, 1)
-            quantise_v(j - 1)
-            if j == 9:
-                scale_h(0)
+            quantise_stage1(0, c - 1)
+            sign_v(1, c, 1, "vector" if c % 2 == 0 else "scalar")
+            if c == 0:
+                load_late_rows()
+            if c > 1:
+                load_next_u()
+        late_bank = turn_banks.tile([P, 512], F32, name="turn")
+        nc.tensor.transpose(out=late_bank[:, 0:P], in_=late_rows[:].bitcast(F32), identity=identity[:])
+        nc.vector.tensor_copy(out=late_cols[:], in_=late_bank[:, 0:56].bitcast(BF16))
+        for b in range(2):
+            nc.vector.tensor_tensor(
+                out=rank_scale[:, 4 * b : 4 * b + 4],
+                in0=late_cols[:, 96 + 8 * b : 100 + 8 * b],
+                in1=late_cols[:, 100 + 8 * b : 104 + 8 * b],
+                op=ALU.mult,
+            )
 
-        for s in range(LAST_SLOT + 1):
-            if s == 0:
-                quantise_x(STEPS - 1)
-                quantise_v(STEPS - 1)
-            quantise_u(s - 1)
-            transpose_u(s + 1)
-            turn_back(s - BACK)
-            if s == 0:
-                stage1_passes(STEPS - 2)
-            if s == 1:
-                stage1_passes(STEPS - 1)
-                group_g(0)
-            stage2_pass(s - RESIDUAL_PASS, 1)
-            stage2_pass(s - MAIN_PASS, 0)
-            sign_u(s)
-            if s == 2:
+        quantise_stage1(0, PASSES - 1)
+        transpose_u(1)
+        for r in range(4):
+            stage1_pass(0, PASSES - 2, r)
+        sign_u(0, "scalar")
+        quantise_stage1(1, 0)
+        transpose_u(2)
+        for r in range(4):
+            stage1_pass(0, PASSES - 1, r)
+        sign_u(1, "scalar")
+        transpose_u(3)
+        done = 2
+        for r in range(4):
+            scale_h(0, r, ("scalar", "vector")[r % 2])
+        for c in range(PASSES):
+            quantise_stage1(1, c + 1)
+            quantise_u(done - 2)
+            for r in range(4):
+                stage1_pass(1, c, r)
+            sign_u(done, "scalar")
+            transpose_u(done + 2)
+            done += 1
+            if c == 1:
+                group_g(0, "vector")
+            if c == 3:
                 quantise_g(0)
-                scale_h(1)
-            if s == 3:
-                group_g(1)
-            if s == 4:
-                quantise_g(1)
-            q = s - SCALE
-            if 0 <= q < TILES and not on_vector(q):
-                scale_main(q)
-            store(s - STORE, "scalar" if s > TILES else "vector")
-            add_residual(s - ADD)
-            if 0 <= q < TILES and on_vector(q):
-                scale_main(q)
+        for r in range(4):
+            scale_h(1, r, ("vector", "scalar")[r % 2])
+        sign_u(done, "scalar")
+        transpose_u(done + 2)
+        done += 1
+        group_g(1, "vector")
+        quantise_u(done - 3)
+        quantise_u(done - 2)
+        quantise_g(1)
+        quantised = done - 1
+
+        for s in range(PAIRS + 3):
+            pair = 2 * (s - 1)
+            for bank_no in range(quantised, done):
+                quantise_u(bank_no)
+            quantised = done
+            scale_main(pair)
+            scale_main(pair + 1)
+            add_residual(pair)
+            add_residual(pair + 1)
+            turn_back(pair - 2)
+            turn_back(pair - 1)
+            for q in (2 * s, 2 * s + 1):
+                for b in range(2):
+                    stage2_pass(q, b)
+            sign_u(done, "scalar")
+            sign_u(done + 1, "vector")
+            transpose_u(done + 2)
+            transpose_u(done + 3)
+            done += 2
+            store(pair - 2, "scalar")
+            store(pair - 1, "vector")

@@ -16,8 +16,7 @@ FLOPS = 2 * 2 * 2 * 512 * 4096 * 512
 P = 128
 PASSES = 8
 TILES = 32
-RAW_TILES = 8
-RAW_U_TILES = 6
+RAW_TILES = 18
 
 PAIRS = TILES // 2
 
@@ -36,7 +35,6 @@ def tile_littlebitlinear_pa_kernel(
     with ExitStack() as ctx:
         const = ctx.enter_context(tc.tile_pool(name="const", bufs=1))
         raw_pool = ctx.enter_context(tc.tile_pool(name="raw_pool", bufs=RAW_TILES))
-        raw_u_pool = ctx.enter_context(tc.tile_pool(name="raw_u_pool", bufs=RAW_U_TILES))
         two = ctx.enter_context(tc.tile_pool(name="two", bufs=2))
         three = ctx.enter_context(tc.tile_pool(name="three", bufs=3))
         four = ctx.enter_context(tc.tile_pool(name="four", bufs=4))
@@ -69,39 +67,45 @@ def tile_littlebitlinear_pa_kernel(
 
         nc.sync.dma_start(out=early_rows[0:16, :], in_=rows_of(v2))
         nc.sync.dma_start(out=early_rows[16:32, :], in_=rows_of(v2_R))
+        nc.gpsimd.dma_start(out=late_rows[0:16, :], in_=rows_of(u1))
+        nc.gpsimd.dma_start(out=late_rows[16:32, :], in_=rows_of(u1_R))
+        nc.gpsimd.dma_start(out=late_rows[32:48, :], in_=bias.rearrange("(r c) -> r c", c=256))
+        nc.gpsimd.dma_start(out=late_rows[48:50, :], in_=rows_of(v1))
+        nc.gpsimd.dma_start(out=late_rows[50:52, :], in_=rows_of(u2))
+        nc.gpsimd.dma_start(out=late_rows[52:54, :], in_=rows_of(v1_R))
+        nc.gpsimd.dma_start(out=late_rows[54:56, :], in_=rows_of(u2_R))
 
+        load_order = []
+        for pair in range(PASSES // 2 + 1):
+            if pair < PASSES // 2:
+                load_order.extend([("x", 0, pair, 0), ("v", 0, pair, 0), ("x", 0, pair, 1), ("v", 0, pair, 1)])
+            if pair > 0:
+                load_order.extend([("v", 1, pair - 1, 0), ("v", 1, pair - 1, 1)])
+        load_order.extend([("u", b, group, 0) for group in range(8) for b in range(2)])
         raw = {}
-        load_order = [(kind, b, c) for c in range(PASSES) for kind, b in (("x", 0), ("v", 0), ("v", 1))]
-        u_load_order = [("u", b, group) for group in range(8) for b in range(2)]
+        in_place = []
+        used_up = set()
 
         def load_next():
             if load_order:
-                kind, b, c = key = load_order.pop(0)
+                kind, b, j, half = key = load_order.pop(0)
+                in_place.append(key)
                 raw[key] = raw_pool.tile([P, 2048], BF16, name="raw")
-                groups = raw[key][:].rearrange("p (r k) -> p r k", r=4)
-                for a in range(2):
-                    src = x_view[:, 2 * a : 2 * a + 2, :] if kind == "x" else v_views[b][a]
-                    nc.sync.dma_start(out=groups[:, 2 * a : 2 * a + 2, :], in_=src[:, :, 512 * c : 512 * (c + 1)])
+                if kind == "u":
+                    src = u_views[b][:, 2 * j : 2 * j + 2, :]
+                else:
+                    rows = x_view[:, 2 * half : 2 * half + 2, :] if kind == "x" else v_views[b][half]
+                    src = rows[:, :, 1024 * j : 1024 * (j + 1)]
+                nc.sync.dma_start(out=raw[key][:].rearrange("p (r k) -> p r k", r=2), in_=src)
 
-        def load_next_u():
-            if u_load_order:
-                kind, b, group = key = u_load_order.pop(0)
-                raw[key] = raw_u_pool.tile([P, 2048], BF16, name="raw_u")
-                nc.sync.dma_start(
-                    out=raw[key][:].rearrange("p (a k) -> p a k", a=2), in_=u_views[b][:, 2 * group : 2 * group + 2, :]
-                )
+        def use_up(key):
+            used_up.add(key)
+            while in_place and in_place[0] in used_up:
+                in_place.pop(0)
+                load_next()
 
         for tile_no in range(RAW_TILES):
             load_next()
-
-        def load_late_rows():
-            nc.sync.dma_start(out=late_rows[0:16, :], in_=rows_of(u1))
-            nc.sync.dma_start(out=late_rows[16:32, :], in_=rows_of(u1_R))
-            nc.sync.dma_start(out=late_rows[32:48, :], in_=bias.rearrange("(r c) -> r c", c=256))
-            nc.sync.dma_start(out=late_rows[48:50, :], in_=rows_of(v1))
-            nc.sync.dma_start(out=late_rows[50:52, :], in_=rows_of(u2))
-            nc.sync.dma_start(out=late_rows[52:54, :], in_=rows_of(v1_R))
-            nc.sync.dma_start(out=late_rows[54:56, :], in_=rows_of(u2_R))
 
         bank = {}
         x_scaled = {}
@@ -120,18 +124,21 @@ def tile_littlebitlinear_pa_kernel(
         turned = {}
 
         def transpose_half(key, half, pool, name):
+            kind, b, c = key
+            raw_key = (kind, b, c, 0) if kind == "u" else (kind, b, c // 2, half)
+            words = raw[raw_key][:].bitcast(F32)
+            first, pitch = (512 * half, 256) if kind == "u" else (256 * (c % 2), 512)
             bank[(key, half)] = pool.tile([P, 512], F32, name=name)
-            words = raw[key][:].bitcast(F32)
             for u in range(2):
                 for r in range(2):
-                    col = (2 * half + r) * 256 + u * P
+                    col = first + r * pitch + u * P
                     nc.tensor.transpose(
                         out=bank[(key, half)][:, u * 256 + r * P : u * 256 + (r + 1) * P],
                         in_=words[:, col : col + P],
                         identity=identity[:],
                     )
-            if half == 1:
-                (load_next_u if key[0] == "u" else load_next)()
+            if (half if kind == "u" else c % 2) == 1:
+                use_up(raw_key)
 
         def by_word(bank_tile):
             return bank_tile[:].bitcast(BF16).rearrange("p (u c e) -> p c u e", u=2, e=2)
@@ -170,14 +177,6 @@ def tile_littlebitlinear_pa_kernel(
                     out=as_words(dst), in0=by_word(bank_tile), scalar1=-TINY, scalar2=TINY, op0=ALU.max, op1=ALU.min
                 )
 
-        def transpose_x(c, half):
-            if c < PASSES:
-                transpose_half(("x", 0, c), half, turn_banks, "turn")
-
-        def transpose_v(b, c, half):
-            if c < PASSES:
-                transpose_half(("v", b, c), half, weight_banks, "weights")
-
         def scale_x(c, half):
             for b in range(2):
                 if half == 0:
@@ -191,7 +190,7 @@ def tile_littlebitlinear_pa_kernel(
                 )
 
         def sign_v(b, c, half, engine):
-            if half == 0:
+            if (b, c) not in signs:
                 signs[(b, c)] = (three, eight)[b].tile([P, 2048], BF16, name="v_signs%d" % b, align_bytes=64)
             take_signs(signs[(b, c)][:, half * 1024 : (half + 1) * 1024], bank[(("v", b, c), half)], engine)
 
@@ -230,14 +229,9 @@ def tile_littlebitlinear_pa_kernel(
         def u_bank(s):
             return (("u", s % 2, s // 4), (s % 4) // 2)
 
-        def transpose_u(s):
-            if s < TILES:
-                transpose_half(u_bank(s)[0], u_bank(s)[1], weight_banks, "weights")
-
         def sign_u(s, engine):
-            if s < TILES:
-                signs[u_bank(s)] = four.tile([P, 1024], BF16, name="u_signs", align_bytes=64)
-                take_signs(signs[u_bank(s)][:], bank[u_bank(s)], engine)
+            signs[u_bank(s)] = four.tile([P, 1024], BF16, name="u_signs", align_bytes=64)
+            take_signs(signs[u_bank(s)][:], bank[u_bank(s)], engine)
 
         def quantise_u(s):
             if 0 <= s < TILES:
@@ -302,85 +296,120 @@ def tile_littlebitlinear_pa_kernel(
         nc.tensor.transpose(out=early_cols[:, 0:P], in_=early_rows[:].bitcast(F32), identity=identity[:])
         nc.vector.tensor_copy(out=v2_words[:], in_=early_cols[:, 0:32])
 
-        transpose_x(0, 0)
-        transpose_v(0, 0, 0)
-        transpose_x(0, 1)
+        v_r = [(("v", 1, c), half) for c in range(PASSES) for half in range(2)]
+        v_r_on_vector = [(("v", 1, c), 1) for c in range(6, PASSES)]
+        v_r_on_scalar = [k for k in v_r if k not in v_r_on_vector]
+        vector_banks = [(("x", 0, c), half) for c in range(PASSES) for half in range(2)] + v_r_on_vector
+        scalar_banks = []
         for c in range(PASSES):
-            transpose_v(0, c, 1)
+            scalar_banks.extend([(("v", 0, c), 0), (("v", 0, c), 1)])
+            scalar_banks.extend([v_r_on_scalar.pop(0) for i in range(1 if c > 1 else 0)])
+        scalar_banks.extend(v_r_on_scalar + [u_bank(s) for s in range(TILES)])
+        signed = []
+
+        def turn_next(stream, turned_banks):
+            if stream:
+                key, half = stream.pop(0)
+                on_scalar = turned_banks is scalar_turned
+                transpose_half(key, half, weight_banks if on_scalar else turn_banks, "weights" if on_scalar else "turn")
+                turned_banks.append((key, half))
+
+        scalar_turned = []
+        vector_turned = []
+
+        def next_on_scalar(engine="scalar"):
+            if scalar_turned:
+                (kind, b, c), half = scalar_turned.pop(0)
+                if kind == "v":
+                    sign_v(b, c, half, engine)
+                else:
+                    sign_u(4 * c + 2 * half + b, engine)
+                signed.append(((kind, b, c), half))
+                turn_next(scalar_banks, scalar_turned)
+
+        def next_on_vector():
+            (kind, b, c), half = vector_turned.pop(0)
+            if kind == "v":
+                sign_v(b, c, half, "vector")
+                signed.append(((kind, b, c), half))
+            else:
+                scale_x(c, half)
+            turn_next(vector_banks, vector_turned)
+
+        def signs_of(b, c):
+            for half in range(2):
+                while (("v", b, c), half) not in signed:
+                    if (("v", b, c), half) in vector_turned + vector_banks:
+                        next_on_vector()
+                    else:
+                        next_on_scalar()
+
+        for i in range(2):
+            turn_next(vector_banks, vector_turned)
+            turn_next(scalar_banks, scalar_turned)
+        for c in range(PASSES):
+            next_on_scalar()
+            next_on_vector()
             for r in range(4):
                 stage1_pass(0, c - 2, r)
-            scale_x(c, 0)
-            sign_v(0, c, 0, "scalar")
-            transpose_v(1, c, 0)
-            transpose_x(c + 1, 0)
-            scale_x(c, 1)
-            sign_v(0, c, 1, "scalar")
-            transpose_v(1, c, 1)
-            transpose_x(c + 1, 1)
-            sign_v(1, c, 0, "scalar")
-            if c < PASSES - 1:
-                transpose_v(0, c + 1, 0)
-            else:
-                transpose_u(0)
+            next_on_scalar()
+            next_on_vector()
             quantise_stage1(0, c - 1)
-            sign_v(1, c, 1, "vector" if c % 2 == 0 else "scalar")
-            if c == 0:
-                load_late_rows()
-            if c > 1:
-                load_next_u()
-        late_bank = turn_banks.tile([P, 512], F32, name="turn")
-        nc.tensor.transpose(out=late_bank[:, 0:P], in_=late_rows[:].bitcast(F32), identity=identity[:])
-        nc.vector.tensor_copy(out=late_cols[:], in_=late_bank[:, 0:56].bitcast(BF16))
-        for b in range(2):
-            nc.vector.tensor_tensor(
-                out=rank_scale[:, 4 * b : 4 * b + 4],
-                in0=late_cols[:, 96 + 8 * b : 100 + 8 * b],
-                in1=late_cols[:, 100 + 8 * b : 104 + 8 * b],
-                op=ALU.mult,
-            )
+            for i in range(1 if c > 1 else 0):
+                next_on_scalar()
+            if c == 1:
+                late_bank = sum_banks.tile([P, 512], F32, name="sums")
+                nc.tensor.transpose(out=late_bank[:, 0:P], in_=late_rows[:].bitcast(F32), identity=identity[:])
+                nc.vector.tensor_copy(out=late_cols[:], in_=late_bank[:, 0:56].bitcast(BF16))
+                for b in range(2):
+                    nc.vector.tensor_tensor(
+                        out=rank_scale[:, 4 * b : 4 * b + 4],
+                        in0=late_cols[:, 96 + 8 * b : 100 + 8 * b],
+                        in1=late_cols[:, 100 + 8 * b : 104 + 8 * b],
+                        op=ALU.mult,
+                    )
 
         quantise_stage1(0, PASSES - 1)
-        transpose_u(1)
         for r in range(4):
             stage1_pass(0, PASSES - 2, r)
-        sign_u(0, "scalar")
+        signs_of(1, 0)
+        next_on_scalar()
         quantise_stage1(1, 0)
-        transpose_u(2)
         for r in range(4):
             stage1_pass(0, PASSES - 1, r)
-        sign_u(1, "scalar")
-        transpose_u(3)
-        done = 2
+        next_on_scalar()
+        signs_of(1, 1)
+        quantise_stage1(1, 1)
         for r in range(4):
-            scale_h(0, r, ("scalar", "vector")[r % 2])
+            scale_h(0, r, "scalar")
         for c in range(PASSES):
-            quantise_stage1(1, c + 1)
-            quantise_u(done - 2)
+            if c + 2 < PASSES:
+                signs_of(1, c + 2)
+                quantise_stage1(1, c + 2)
             for r in range(4):
                 stage1_pass(1, c, r)
-            sign_u(done, "scalar")
-            transpose_u(done + 2)
-            done += 1
-            if c == 1:
+            if c > 3:
+                next_on_scalar()
+            if c == 2:
                 group_g(0, "vector")
-            if c == 3:
+            if c == 2 + 2:
                 quantise_g(0)
         for r in range(4):
             scale_h(1, r, ("vector", "scalar")[r % 2])
-        sign_u(done, "scalar")
-        transpose_u(done + 2)
-        done += 1
+        for i in range(1):
+            next_on_scalar()
         group_g(1, "vector")
-        quantise_u(done - 3)
-        quantise_u(done - 2)
+        quantised = 0
+        while u_bank(quantised + 1) in signed:
+            quantise_u(quantised)
+            quantised += 1
         quantise_g(1)
-        quantised = done - 1
 
         for s in range(PAIRS + 3):
             pair = 2 * (s - 1)
-            for bank_no in range(quantised, done):
-                quantise_u(bank_no)
-            quantised = done
+            while quantised < TILES and u_bank(quantised) in signed:
+                quantise_u(quantised)
+                quantised += 1
             scale_main(pair)
             scale_main(pair + 1)
             add_residual(pair)
@@ -390,10 +419,7 @@ def tile_littlebitlinear_pa_kernel(
             for q in (2 * s, 2 * s + 1):
                 for b in range(2):
                     stage2_pass(q, b)
-            sign_u(done, "scalar")
-            sign_u(done + 1, "vector")
-            transpose_u(done + 2)
-            transpose_u(done + 3)
-            done += 2
+            next_on_scalar("vector" if s % 2 else "scalar")
+            next_on_scalar("vector")
             store(pair - 2, "scalar")
-            store(pair - 1, "vector")
+            store(pair - 1, "scalar")

@@ -38,9 +38,10 @@ def tile_littlebitlinear_pa_kernel(
         two = ctx.enter_context(tc.tile_pool(name="two", bufs=2))
         three = ctx.enter_context(tc.tile_pool(name="three", bufs=3))
         four = ctx.enter_context(tc.tile_pool(name="four", bufs=4))
+        five = ctx.enter_context(tc.tile_pool(name="five", bufs=5))
         six = ctx.enter_context(tc.tile_pool(name="six", bufs=6))
         eight = ctx.enter_context(tc.tile_pool(name="eight", bufs=8))
-        twenty = ctx.enter_context(tc.tile_pool(name="twenty", bufs=20))
+        twenty = ctx.enter_context(tc.tile_pool(name="twenty", bufs=18))
         weight_banks = ctx.enter_context(tc.psum_pool(name="weight_banks", bufs=2))
         turn_banks = ctx.enter_context(tc.psum_pool(name="turn_banks", bufs=2))
         sum_banks = ctx.enter_context(tc.psum_pool(name="sum_banks", bufs=4))
@@ -67,13 +68,15 @@ def tile_littlebitlinear_pa_kernel(
 
         nc.sync.dma_start(out=early_rows[0:16, :], in_=rows_of(v2))
         nc.sync.dma_start(out=early_rows[16:32, :], in_=rows_of(v2_R))
-        nc.gpsimd.dma_start(out=late_rows[0:16, :], in_=rows_of(u1))
-        nc.gpsimd.dma_start(out=late_rows[16:32, :], in_=rows_of(u1_R))
-        nc.gpsimd.dma_start(out=late_rows[32:48, :], in_=bias.rearrange("(r c) -> r c", c=256))
-        nc.gpsimd.dma_start(out=late_rows[48:50, :], in_=rows_of(v1))
-        nc.gpsimd.dma_start(out=late_rows[50:52, :], in_=rows_of(u2))
-        nc.gpsimd.dma_start(out=late_rows[52:54, :], in_=rows_of(v1_R))
-        nc.gpsimd.dma_start(out=late_rows[54:56, :], in_=rows_of(u2_R))
+        late_loads = [
+            (late_rows[0:16, :], rows_of(u1)),
+            (late_rows[16:32, :], rows_of(u1_R)),
+            (late_rows[32:48, :], bias.rearrange("(r c) -> r c", c=256)),
+            (late_rows[48:50, :], rows_of(v1)),
+            (late_rows[50:52, :], rows_of(u2)),
+            (late_rows[52:54, :], rows_of(v1_R)),
+            (late_rows[54:56, :], rows_of(u2_R)),
+        ]
 
         load_order = []
         for pair in range(PASSES // 2 + 1):
@@ -106,6 +109,9 @@ def tile_littlebitlinear_pa_kernel(
 
         for tile_no in range(RAW_TILES):
             load_next()
+            if tile_no > 3 and late_loads:
+                dst, src = late_loads.pop()
+                nc.sync.dma_start(out=dst, in_=src)
 
         bank = {}
         x_scaled = {}
@@ -245,7 +251,7 @@ def tile_littlebitlinear_pa_kernel(
 
         def scale_main(q):
             if 0 <= q < TILES:
-                scaled[q] = three.tile([P, 512], F32, name="scaled")
+                scaled[q] = five.tile([P, 512], F32, name="scaled")
                 nc.scalar.activation(
                     out=scaled[q][:],
                     in_=y_main[q][:],
@@ -300,6 +306,7 @@ def tile_littlebitlinear_pa_kernel(
         v_r_on_vector = [(("v", 1, c), 1) for c in range(6, PASSES)]
         v_r_on_scalar = [k for k in v_r if k not in v_r_on_vector]
         vector_banks = [(("x", 0, c), half) for c in range(PASSES) for half in range(2)] + v_r_on_vector
+        vector_banks.insert(8, (("late", 0, 0), 0))
         scalar_banks = []
         for c in range(PASSES):
             scalar_banks.extend([(("v", 0, c), 0), (("v", 0, c), 1)])
@@ -307,11 +314,25 @@ def tile_littlebitlinear_pa_kernel(
         scalar_banks.extend(v_r_on_scalar + [u_bank(s) for s in range(TILES)])
         signed = []
 
+        def spread_vectors(late_bank):
+            nc.vector.tensor_copy(out=late_cols[:], in_=late_bank[:, 0:56].bitcast(BF16))
+            for b in range(2):
+                nc.vector.tensor_tensor(
+                    out=rank_scale[:, 4 * b : 4 * b + 4],
+                    in0=late_cols[:, 96 + 8 * b : 100 + 8 * b],
+                    in1=late_cols[:, 100 + 8 * b : 104 + 8 * b],
+                    op=ALU.mult,
+                )
+
         def turn_next(stream, turned_banks):
             if stream:
                 key, half = stream.pop(0)
                 on_scalar = turned_banks is scalar_turned
-                transpose_half(key, half, weight_banks if on_scalar else turn_banks, "weights" if on_scalar else "turn")
+                if key[0] == "late":
+                    bank[(key, half)] = turn_banks.tile([P, 512], F32, name="turn")
+                    nc.tensor.transpose(out=bank[(key, half)][:, 0:P], in_=late_rows[:].bitcast(F32), identity=identity[:])
+                else:
+                    transpose_half(key, half, weight_banks if on_scalar else turn_banks, "weights" if on_scalar else "turn")
                 turned_banks.append((key, half))
 
         scalar_turned = []
@@ -332,9 +353,13 @@ def tile_littlebitlinear_pa_kernel(
             if kind == "v":
                 sign_v(b, c, half, "vector")
                 signed.append(((kind, b, c), half))
-            else:
+            elif kind == "x":
                 scale_x(c, half)
+            else:
+                spread_vectors(bank[((kind, b, c), half)])
             turn_next(vector_banks, vector_turned)
+            if vector_turned and vector_turned[0][0][0] == "late":
+                next_on_vector()
 
         def signs_of(b, c):
             for half in range(2):
@@ -357,17 +382,6 @@ def tile_littlebitlinear_pa_kernel(
             quantise_stage1(0, c - 1)
             for i in range(1 if c > 1 else 0):
                 next_on_scalar()
-            if c == 1:
-                late_bank = sum_banks.tile([P, 512], F32, name="sums")
-                nc.tensor.transpose(out=late_bank[:, 0:P], in_=late_rows[:].bitcast(F32), identity=identity[:])
-                nc.vector.tensor_copy(out=late_cols[:], in_=late_bank[:, 0:56].bitcast(BF16))
-                for b in range(2):
-                    nc.vector.tensor_tensor(
-                        out=rank_scale[:, 4 * b : 4 * b + 4],
-                        in0=late_cols[:, 96 + 8 * b : 100 + 8 * b],
-                        in1=late_cols[:, 100 + 8 * b : 104 + 8 * b],
-                        op=ALU.mult,
-                    )
 
         quantise_stage1(0, PASSES - 1)
         for r in range(4):
@@ -398,28 +412,32 @@ def tile_littlebitlinear_pa_kernel(
             scale_h(1, r, ("vector", "scalar")[r % 2])
         for i in range(1):
             next_on_scalar()
-        group_g(1, "vector")
         quantised = 0
+        quantise_u(0)
+        quantise_u(1)
+        group_g(1, "vector")
+        stage2_pass(0, 0)
+        stage2_pass(1, 0)
+        quantised = 2
         while u_bank(quantised + 1) in signed:
             quantise_u(quantised)
             quantised += 1
         quantise_g(1)
 
         for s in range(PAIRS + 3):
-            pair = 2 * (s - 1)
+            pair = 2 * s
             while quantised < TILES and u_bank(quantised) in signed:
                 quantise_u(quantised)
                 quantised += 1
             scale_main(pair)
             scale_main(pair + 1)
-            add_residual(pair)
-            add_residual(pair + 1)
-            turn_back(pair - 2)
-            turn_back(pair - 1)
-            for q in (2 * s, 2 * s + 1):
-                for b in range(2):
-                    stage2_pass(q, b)
+            add_residual(pair - 2)
+            add_residual(pair - 1)
+            turn_back(pair - 4)
+            turn_back(pair - 3)
+            for q, b in ((pair + 2, 0), (pair + 3, 0), (pair, 1), (pair + 1, 1)):
+                stage2_pass(q, b)
             next_on_scalar("vector" if s % 2 else "scalar")
             next_on_scalar("vector")
-            store(pair - 2, "scalar")
-            store(pair - 1, "scalar")
+            store(pair - 4, "scalar")
+            store(pair - 3, "vector" if not scalar_turned else "scalar")

@@ -375,10 +375,12 @@ def tile_littlebitlinear_pa_kernel(
         for c in range(PASSES):
             next_on_scalar()
             next_on_vector()
-            for r in range(4):
+            for r in (0, 1):
                 stage1_pass(0, c - 2, r)
             next_on_scalar()
             next_on_vector()
+            for r in (2, 3):
+                stage1_pass(0, c - 2, r)
             quantise_stage1(0, c - 1)
             for i in range(1 if c > 1 else 0):
                 next_on_scalar()

@@ -45,7 +45,6 @@ def tile_littlebitlinear_pa_kernel(
         weight_banks = ctx.enter_context(tc.psum_pool(name="weight_banks", bufs=2))
         turn_banks = ctx.enter_context(tc.psum_pool(name="turn_banks", bufs=2))
         sum_banks = ctx.enter_context(tc.psum_pool(name="sum_banks", bufs=4))
-        ctx.enter_context(tc.manual_schedule())
 
         identity = const.tile([P, P], F32, name="identity")
         make_identity(nc, identity[:])

@@ -20,6 +20,7 @@ RAW_TILES = 18
 
 PAIRS = TILES // 2
 
+BOTH = 2
 TINY = 2.0 ** -119
 
 
@@ -39,9 +40,8 @@ def tile_littlebitlinear_pa_kernel(
         three = ctx.enter_context(tc.tile_pool(name="three", bufs=3))
         four = ctx.enter_context(tc.tile_pool(name="four", bufs=4))
         five = ctx.enter_context(tc.tile_pool(name="five", bufs=5))
-        six = ctx.enter_context(tc.tile_pool(name="six", bufs=6))
         eight = ctx.enter_context(tc.tile_pool(name="eight", bufs=8))
-        twenty = ctx.enter_context(tc.tile_pool(name="twenty", bufs=18))
+        twenty = ctx.enter_context(tc.tile_pool(name="twenty", bufs=20))
         weight_banks = ctx.enter_context(tc.psum_pool(name="weight_banks", bufs=2))
         turn_banks = ctx.enter_context(tc.psum_pool(name="turn_banks", bufs=2))
         sum_banks = ctx.enter_context(tc.psum_pool(name="sum_banks", bufs=4))
@@ -79,8 +79,11 @@ def tile_littlebitlinear_pa_kernel(
 
         load_order = []
         for pair in range(PASSES // 2 + 1):
-            if pair < PASSES // 2:
-                load_order.extend([("x", 0, pair, 0), ("v", 0, pair, 0), ("x", 0, pair, 1), ("v", 0, pair, 1)])
+            if pair < 1:
+                for c in (2 * pair, 2 * pair + 1):
+                    load_order.extend([("x", 0, c, BOTH), ("v", 0, c, BOTH)])
+            elif pair < PASSES // 2:
+                load_order.extend([("x", 0, pair, 0), ("x", 0, pair, 1), ("v", 0, pair, 0), ("v", 0, pair, 1)])
             if pair > 0:
                 load_order.extend([("v", 1, pair - 1, 0), ("v", 1, pair - 1, 1)])
         load_order.extend([("u", b, group, 0) for group in range(8) for b in range(2)])
@@ -93,6 +96,14 @@ def tile_littlebitlinear_pa_kernel(
                 kind, b, j, half = key = load_order.pop(0)
                 in_place.append(key)
                 raw[key] = raw_pool.tile([P, 2048], BF16, name="raw")
+                if half == BOTH:
+                    for a in range(2):
+                        rows = x_view[:, 2 * a : 2 * a + 2, :] if kind == "x" else v_views[b][a]
+                        nc.sync.dma_start(
+                            out=raw[key][:, 1024 * a : 1024 * (a + 1)].rearrange("p (r k) -> p r k", r=2),
+                            in_=rows[:, :, 512 * j : 512 * (j + 1)],
+                        )
+                    return
                 if kind == "u":
                     src = u_views[b][:, 2 * j : 2 * j + 2, :]
                 else:
@@ -130,9 +141,13 @@ def tile_littlebitlinear_pa_kernel(
 
         def transpose_half(key, half, pool, name):
             kind, b, c = key
-            raw_key = (kind, b, c, 0) if kind == "u" else (kind, b, c // 2, half)
+            if (kind, b, c, BOTH) in raw:
+                raw_key, first, pitch, last = (kind, b, c, BOTH), 512 * half, 256, half == 1
+            elif kind == "u":
+                raw_key, first, pitch, last = (kind, b, c, 0), 512 * half, 256, half == 1
+            else:
+                raw_key, first, pitch, last = (kind, b, c // 2, half), 256 * (c % 2), 512, c % 2 == 1
             words = raw[raw_key][:].bitcast(F32)
-            first, pitch = (512 * half, 256) if kind == "u" else (256 * (c % 2), 512)
             bank[(key, half)] = pool.tile([P, 512], F32, name=name)
             for u in range(2):
                 for r in range(2):
@@ -142,7 +157,7 @@ def tile_littlebitlinear_pa_kernel(
                         in_=words[:, col : col + P],
                         identity=identity[:],
                     )
-            if (half if kind == "u" else c % 2) == 1:
+            if last:
                 use_up(raw_key)
 
         def by_word(bank_tile):
@@ -261,7 +276,7 @@ def tile_littlebitlinear_pa_kernel(
 
         def add_residual(q):
             if 0 <= q < TILES:
-                result[q] = six.tile([P, 512], F32, name="result")
+                result[q] = eight.tile([P, 512], F32, name="x_scaled1", align_bytes=64)
                 nc.vector.scalar_tensor_tensor(
                     out=result[q][:],
                     in0=y_residual[q][:],
@@ -285,7 +300,7 @@ def tile_littlebitlinear_pa_kernel(
 
         def store(q, engine):
             if 0 <= q < TILES:
-                rows = four.tile([P, 512], F32, name="rows")
+                rows = eight.tile([P, 512], F32, name="v_signs1", align_bytes=64)
                 dst = rows[:].rearrange("p (i m e) -> p i m e", i=2, e=2)
                 src = turned[q][:].rearrange("p (i e m) -> p i m e", i=2, e=2)
                 if engine == "scalar":

@@ -20,7 +20,6 @@ RAW_TILES = 18
 
 PAIRS = TILES // 2
 
-BOTH = 2
 TINY = 2.0 ** -119
 
 
@@ -51,7 +50,8 @@ def tile_littlebitlinear_pa_kernel(
 
         early_rows = const.tile([P, 256], BF16, name="early_rows")
         late_rows = const.tile([P, 256], BF16, name="late_rows")
-        nc.vector.memset(early_rows[:].bitcast(F32), 0.0)
+        nc.vector.memset(early_rows[32:64, :].bitcast(F32), 0.0)
+        nc.vector.memset(early_rows[64:P, :].bitcast(F32), 0.0)
         nc.vector.memset(late_rows[:].bitcast(F32), 0.0)
         ones = const.tile([P, 512], BF16, name="ones", align_bytes=64)
         nc.vector.memset(ones[:], 1.0)
@@ -79,11 +79,8 @@ def tile_littlebitlinear_pa_kernel(
 
         load_order = []
         for pair in range(PASSES // 2 + 1):
-            if pair < 1:
-                for c in (2 * pair, 2 * pair + 1):
-                    load_order.extend([("x", 0, c, BOTH), ("v", 0, c, BOTH)])
-            elif pair < PASSES // 2:
-                load_order.extend([("x", 0, pair, 0), ("x", 0, pair, 1), ("v", 0, pair, 0), ("v", 0, pair, 1)])
+            if pair < PASSES // 2:
+                load_order.extend([("x", 0, pair, 0), ("v", 0, pair, 0), ("x", 0, pair, 1), ("v", 0, pair, 1)])
             if pair > 0:
                 load_order.extend([("v", 1, pair - 1, 0), ("v", 1, pair - 1, 1)])
         load_order.extend([("u", b, group, 0) for group in range(8) for b in range(2)])
@@ -96,14 +93,6 @@ def tile_littlebitlinear_pa_kernel(
                 kind, b, j, half = key = load_order.pop(0)
                 in_place.append(key)
                 raw[key] = raw_pool.tile([P, 2048], BF16, name="raw")
-                if half == BOTH:
-                    for a in range(2):
-                        rows = x_view[:, 2 * a : 2 * a + 2, :] if kind == "x" else v_views[b][a]
-                        nc.sync.dma_start(
-                            out=raw[key][:, 1024 * a : 1024 * (a + 1)].rearrange("p (r k) -> p r k", r=2),
-                            in_=rows[:, :, 512 * j : 512 * (j + 1)],
-                        )
-                    return
                 if kind == "u":
                     src = u_views[b][:, 2 * j : 2 * j + 2, :]
                 else:
@@ -141,9 +130,7 @@ def tile_littlebitlinear_pa_kernel(
 
         def transpose_half(key, half, pool, name):
             kind, b, c = key
-            if (kind, b, c, BOTH) in raw:
-                raw_key, first, pitch, last = (kind, b, c, BOTH), 512 * half, 256, half == 1
-            elif kind == "u":
+            if kind == "u":
                 raw_key, first, pitch, last = (kind, b, c, 0), 512 * half, 256, half == 1
             else:
                 raw_key, first, pitch, last = (kind, b, c // 2, half), 256 * (c % 2), 512, c % 2 == 1
@@ -216,8 +203,8 @@ def tile_littlebitlinear_pa_kernel(
 
         def quantise_stage1(b, c):
             if 0 <= c < PASSES:
-                x_codes[(b, c)] = quantise(x_scaled[(b, c)], 512, three, "x")
-                w_codes[(b, c)] = quantise_signs(signs[(b, c)], 512, three, "v")
+                x_codes[(b, c)] = quantise(x_scaled[(b, c)], 512, four, "x")
+                w_codes[(b, c)] = quantise_signs(signs[(b, c)], 512, four, "v")
 
         def stage1_pass(b, c, r):
             if 0 <= c < PASSES:
@@ -317,7 +304,7 @@ def tile_littlebitlinear_pa_kernel(
         nc.vector.tensor_copy(out=v2_words[:], in_=early_cols[:, 0:32])
 
         v_r = [(("v", 1, c), half) for c in range(PASSES) for half in range(2)]
-        v_r_on_vector = [(("v", 1, c), 1) for c in range(6, PASSES)]
+        v_r_on_vector = [(("v", 1, c), 1) for c in range(4, PASSES)]
         v_r_on_scalar = [k for k in v_r if k not in v_r_on_vector]
         vector_banks = [(("x", 0, c), half) for c in range(PASSES) for half in range(2)] + v_r_on_vector
         vector_banks.insert(8, (("late", 0, 0), 0))

@@ -108,7 +108,7 @@ def tile_littlebitlinear_pa_kernel(
 
         for tile_no in range(RAW_TILES):
             load_next()
-            if tile_no > 3 and late_loads:
+            if tile_no > 10 and late_loads:
                 dst, src = late_loads.pop()
                 nc.sync.dma_start(out=dst, in_=src)
 
@@ -306,8 +306,7 @@ def tile_littlebitlinear_pa_kernel(
         v_r = [(("v", 1, c), half) for c in range(PASSES) for half in range(2)]
         v_r_on_vector = [(("v", 1, c), 1) for c in range(4, PASSES)]
         v_r_on_scalar = [k for k in v_r if k not in v_r_on_vector]
-        vector_banks = [(("x", 0, c), half) for c in range(PASSES) for half in range(2)] + v_r_on_vector
-        vector_banks.insert(8, (("late", 0, 0), 0))
+        vector_banks = [(("x", 0, c), half) for c in range(PASSES) for half in range(2)] + [(("late", 0, 0), 0)] + v_r_on_vector
         scalar_banks = []
         for c in range(PASSES):
             scalar_banks.extend([(("v", 0, c), 0), (("v", 0, c), 1)])

from contextlib import ExitStack

import concourse.mybir as mybir
from concourse.masks import make_identity

F32 = mybir.dt.float32
BF16 = mybir.dt.bfloat16
U32 = mybir.dt.uint32
U8 = mybir.dt.uint8
FP8X4 = mybir.dt.float8_e4m3fn_x4
ACT = mybir.ActivationFunctionType
ALU = mybir.AluOpType

FLOPS = 2 * 2 * 2 * 512 * 4096 * 512

P = 128
PASSES = 8
TILES = 32
RAW_TILES = 18

PAIRS = TILES // 2

TINY = 2.0 ** -119


def tile_littlebitlinear_pa_kernel(
    tc, x, V, U, v1, v2, u1, u2, V_R, U_R, v1_R, v2_R, u1_R, u2_R, bias, out
):
    nc = tc.nc
    x_view = x.flatten_outer_dims().rearrange("(i p) k -> p i k", p=P)
    out_view = out.flatten_outer_dims().rearrange("(i p) o -> p i o", p=P)
    v_views = [m.rearrange("(a p e) k -> a p e k", a=2, p=P, e=2) for m in (V, V_R)]
    u_views = [m.rearrange("(a p e) s -> p a (e s)", p=P, e=2) for m in (U, U_R)]

    with ExitStack() as ctx:
        const = ctx.enter_context(tc.tile_pool(name="const", bufs=1))
        raw_pool = ctx.enter_context(tc.tile_pool(name="raw_pool", bufs=RAW_TILES))
        two = ctx.enter_context(tc.tile_pool(name="two", bufs=2))
        three = ctx.enter_context(tc.tile_pool(name="three", bufs=3))
        four = ctx.enter_context(tc.tile_pool(name="four", bufs=4))
        five = ctx.enter_context(tc.tile_pool(name="five", bufs=5))
        eight = ctx.enter_context(tc.tile_pool(name="eight", bufs=8))
        twenty = ctx.enter_context(tc.tile_pool(name="twenty", bufs=20))
        weight_banks = ctx.enter_context(tc.psum_pool(name="weight_banks", bufs=2))
        turn_banks = ctx.enter_context(tc.psum_pool(name="turn_banks", bufs=2))
        sum_banks = ctx.enter_context(tc.psum_pool(name="sum_banks", bufs=4))

        identity = const.tile([P, P], F32, name="identity")
        make_identity(nc, identity[:])

        early_rows = const.tile([P, 256], BF16, name="early_rows")
        late_rows = const.tile([P, 256], BF16, name="late_rows")
        nc.vector.memset(early_rows[32:64, :].bitcast(F32), 0.0)
        nc.vector.memset(early_rows[64:P, :].bitcast(F32), 0.0)
        nc.vector.memset(late_rows[:].bitcast(F32), 0.0)
        ones = const.tile([P, 512], BF16, name="ones", align_bytes=64)
        nc.vector.memset(ones[:], 1.0)
        ones_codes = const.tile([P, P], U32, name="ones_codes", align_bytes=64)
        ones_scales = const.tile([P, P], U8, name="ones_scales", align_bytes=64)
        nc.vector.quantize_mx(out=ones_codes[:].bitcast(FP8X4), scales=ones_scales[:], in_=ones[:])
        v2_words = const.tile([P, 32], F32, name="v2_words")
        late_cols = const.tile([P, 112], F32, name="late_cols")
        rank_scale = const.tile([P, 8], F32, name="rank_scale")

        def rows_of(vec):
            return vec.rearrange("o (r c) -> (o r) c", c=256)

        nc.sync.dma_start(out=early_rows[0:16, :], in_=rows_of(v2))
        nc.sync.dma_start(out=early_rows[16:32, :], in_=rows_of(v2_R))
        late_loads = [
            (late_rows[0:16, :], rows_of(u1)),
            (late_rows[16:32, :], rows_of(u1_R)),
            (late_rows[32:48, :], bias.rearrange("(r c) -> r c", c=256)),
            (late_rows[48:50, :], rows_of(v1)),
            (late_rows[50:52, :], rows_of(u2)),
            (late_rows[52:54, :], rows_of(v1_R)),
            (late_rows[54:56, :], rows_of(u2_R)),
        ]

        load_order = []
        for pair in range(PASSES // 2 + 1):
            if pair < PASSES // 2:
                load_order.extend([("x", 0, pair, 0), ("v", 0, pair, 0), ("x", 0, pair, 1), ("v", 0, pair, 1)])
            if pair > 0:
                load_order.extend([("v", 1, pair - 1, 0), ("v", 1, pair - 1, 1)])
        load_order.extend([("u", b, group, 0) for group in range(8) for b in range(2)])
        raw = {}
        in_place = []
        used_up = set()

        def load_next():
            if load_order:
                kind, b, j, half = key = load_order.pop(0)
                in_place.append(key)
                raw[key] = raw_pool.tile([P, 2048], BF16, name="raw")
                if kind == "u":
                    src = u_views[b][:, 2 * j : 2 * j + 2, :]
                else:
                    rows = x_view[:, 2 * half : 2 * half + 2, :] if kind == "x" else v_views[b][half]
                    src = rows[:, :, 1024 * j : 1024 * (j + 1)]
                nc.sync.dma_start(out=raw[key][:].rearrange("p (r k) -> p r k", r=2), in_=src)

        def use_up(key):
            used_up.add(key)
            while in_place and in_place[0] in used_up:
                in_place.pop(0)
                load_next()

        for tile_no in range(RAW_TILES):
            load_next()
            if tile_no > 10 and late_loads:
                dst, src = late_loads.pop()
                nc.sync.dma_start(out=dst, in_=src)

        bank = {}
        x_scaled = {}
        signs = {}
        x_codes = {}
        w_codes = {}
        u_codes = {}
        g_codes = {}
        h_sum = {}
        g_planes = {}
        g_grouped = {}
        y_main = {}
        y_residual = {}
        scaled = {}
        result = {}
        turned = {}

        def transpose_half(key, half, pool, name):
            kind, b, c = key
            if kind == "u":
                raw_key, first, pitch, last = (kind, b, c, 0), 512 * half, 256, half == 1
            else:
                raw_key, first, pitch, last = (kind, b, c // 2, half), 256 * (c % 2), 512, c % 2 == 1
            words = raw[raw_key][:].bitcast(F32)
            bank[(key, half)] = pool.tile([P, 512], F32, name=name)
            for u in range(2):
                for r in range(2):
                    col = first + r * pitch + u * P
                    nc.tensor.transpose(
                        out=bank[(key, half)][:, u * 256 + r * P : u * 256 + (r + 1) * P],
                        in_=words[:, col : col + P],
                        identity=identity[:],
                    )
            if last:
                use_up(raw_key)

        def by_word(bank_tile):
            return bank_tile[:].bitcast(BF16).rearrange("p (u c e) -> p c u e", u=2, e=2)

        def as_words(ap):
            return ap.rearrange("p (c u e) -> p c u e", u=2, e=2)

        def quantise(src, width, pool, name):
            codes = pool.tile([P, width], U32, name=name + "_codes", align_bytes=64)
            scales = pool.tile([P, width], U8, name=name + "_scales", align_bytes=64)
            nc.vector.quantize_mx(out=codes[:].bitcast(FP8X4), scales=scales[:], in_=src[:])
            return (codes, scales)

        def quantise_signs(src, width, pool, name):
            codes = pool.tile([P, width], U32, name=name + "_codes", align_bytes=64)
            unused = two.tile([P, 512], U8, name="unused", align_bytes=64)
            nc.vector.quantize_mx(out=codes[:].bitcast(FP8X4), scales=unused[:, 0:width], in_=src[:])
            return codes

        def mx_pass(dst, weights, col, moving, start, stop):
            nc.tensor.matmul_mx(
                out=dst[:],
                lhsT=weights[:, col * P : (col + 1) * P].bitcast(FP8X4),
                lhsT_scale=ones_scales[:],
                rhs=moving[0][:].bitcast(FP8X4),
                rhs_scale=moving[1][:],
                start=start,
                stop=stop,
            )

        def take_signs(dst, bank_tile, engine):
            if engine == "scalar":
                nc.scalar.activation(out=as_words(dst), in_=by_word(bank_tile), func=ACT.Sign)
            else:
                nc.vector.tensor_scalar(
                    out=as_words(dst), in0=by_word(bank_tile), scalar1=-TINY, scalar2=TINY, op0=ALU.max, op1=ALU.min
                )

        def scale_x(c, half):
            for b in range(2):
                if half == 0:
                    x_scaled[(b, c)] = (two, eight)[b].tile([P, 2048], BF16, name="x_scaled%d" % b, align_bytes=64)
                v2_of_word = v2_words[:].bitcast(BF16)[:, 32 * b + 4 * c : 32 * b + 4 * c + 4]
                nc.vector.tensor_tensor(
                    out=as_words(x_scaled[(b, c)][:, half * 1024 : (half + 1) * 1024]),
                    in0=by_word(bank[(("x", 0, c), half)]),
                    in1=v2_of_word.rearrange("p (u e) -> p u e", u=2).unsqueeze(1).to_broadcast([P, 256, 2, 2]),
                    op=ALU.mult,
                )

        def sign_v(b, c, half, engine):
            if (b, c) not in signs:
                signs[(b, c)] = (three, eight)[b].tile([P, 2048], BF16, name="v_signs%d" % b, align_bytes=64)
            take_signs(signs[(b, c)][:, half * 1024 : (half + 1) * 1024], bank[(("v", b, c), half)], engine)

        def quantise_stage1(b, c):
            if 0 <= c < PASSES:
                x_codes[(b, c)] = quantise(x_scaled[(b, c)], 512, four, "x")
                w_codes[(b, c)] = quantise_signs(signs[(b, c)], 512, four, "v")

        def stage1_pass(b, c, r):
            if 0 <= c < PASSES:
                if c == 0:
                    h_sum[(b, r)] = sum_banks.tile([P, 512], F32, name="sums")
                mx_pass(h_sum[(b, r)], w_codes[(b, c)], r, x_codes[(b, c)], c == 0, c == PASSES - 1)

        def scale_h(b, r, engine):
            if r == 0:
                g_planes[b] = two.tile([P, 4, 512], BF16, name="x_scaled0", align_bytes=64)
            column = rank_scale[:, 4 * b + r : 4 * b + r + 1]
            if engine == "scalar":
                nc.scalar.activation(out=g_planes[b][:, r, :], in_=h_sum[(b, r)][:], func=ACT.Copy, scale=column)
            else:
                nc.vector.tensor_scalar(out=g_planes[b][:, r, :], in0=h_sum[(b, r)][:], scalar1=column, scalar2=None, op0=ALU.mult)

        def group_g(b, engine):
            g_grouped[b] = three.tile([P, 2048], BF16, name="v_signs0", align_bytes=64)
            dst = g_grouped[b][:].rearrange("p (n t) -> p n t", t=4)
            src = g_planes[b][:].rearrange("p t n -> p n t")
            if engine == "scalar":
                nc.scalar.copy(out=dst, in_=src)
            else:
                nc.vector.tensor_copy(out=dst, in_=src)

        def quantise_g(b):
            g_codes[b] = quantise(g_grouped[b], 512, const, "g%d" % b)

        def u_bank(s):
            return (("u", s % 2, s // 4), (s % 4) // 2)

        def sign_u(s, engine):
            signs[u_bank(s)] = four.tile([P, 1024], BF16, name="u_signs", align_bytes=64)
            take_signs(signs[u_bank(s)][:], bank[u_bank(s)], engine)

        def quantise_u(s):
            if 0 <= s < TILES:
                u_codes[u_bank(s)] = quantise_signs(signs[u_bank(s)], 256, twenty, "u")

        def stage2_pass(q, b):
            if q < TILES:
                sums = sum_banks.tile([P, 512], F32, name="sums")
                (y_main if b == 0 else y_residual)[q] = sums
                mx_pass(sums, u_codes[(("u", b, q // 4), (q % 4) // 2)], q % 2, g_codes[b], True, True)

        def scale_main(q):
            if 0 <= q < TILES:
                scaled[q] = five.tile([P, 512], F32, name="scaled")
                nc.scalar.activation(
                    out=scaled[q][:],
                    in_=y_main[q][:],
                    func=ACT.Identity,
                    scale=late_cols[:, q : q + 1],
                    bias=late_cols[:, 64 + q : 65 + q],
                )

        def add_residual(q):
            if 0 <= q < TILES:
                result[q] = eight.tile([P, 512], F32, name="x_scaled1", align_bytes=64)
                nc.vector.scalar_tensor_tensor(
                    out=result[q][:],
                    in0=y_residual[q][:],
                    scalar=late_cols[:, 32 + q : 33 + q],
                    in1=scaled[q][:],
                    op0=ALU.mult,
                    op1=ALU.add,
                )

        def turn_back(q):
            if 0 <= q < TILES:
                turned[q] = turn_banks.tile([P, 512], F32, name="turn")
                for i in range(2):
                    for e in range(2):
                        tokens = (2 * (q % 2) + i) * P
                        nc.tensor.transpose(
                            out=turned[q][:, (2 * i + e) * P : (2 * i + e + 1) * P],
                            in_=result[2 * (q // 2) + e][:, tokens : tokens + P],
                            identity=identity[:],
                        )

        def store(q, engine):
            if 0 <= q < TILES:
                rows = eight.tile([P, 512], F32, name="v_signs1", align_bytes=64)
                dst = rows[:].rearrange("p (i m e) -> p i m e", i=2, e=2)
                src = turned[q][:].rearrange("p (i e m) -> p i m e", i=2, e=2)
                if engine == "scalar":
                    nc.scalar.copy(out=dst, in_=src)
                else:
                    nc.vector.tensor_copy(out=dst, in_=src)
                nc.sync.dma_start(
                    out=out_view[:, 2 * (q % 2) : 2 * (q % 2) + 2, (q // 2) * 256 : (q // 2 + 1) * 256],
                    in_=rows[:].rearrange("p (i o) -> p i o", i=2),
                )

        early_cols = turn_banks.tile([P, 512], F32, name="turn")
        nc.tensor.transpose(out=early_cols[:, 0:P], in_=early_rows[:].bitcast(F32), identity=identity[:])
        nc.vector.tensor_copy(out=v2_words[:], in_=early_cols[:, 0:32])

        v_r = [(("v", 1, c), half) for c in range(PASSES) for half in range(2)]
        v_r_on_vector = [(("v", 1, c), 1) for c in range(4, PASSES)]
        v_r_on_scalar = [k for k in v_r if k not in v_r_on_vector]
        vector_banks = [(("x", 0, c), half) for c in range(PASSES) for half in range(2)] + [(("late", 0, 0), 0)] + v_r_on_vector
        scalar_banks = []
        for c in range(PASSES):
            scalar_banks.extend([(("v", 0, c), 0), (("v", 0, c), 1)])
            scalar_banks.extend([v_r_on_scalar.pop(0) for i in range(1 if c > 1 else 0)])
        scalar_banks.extend(v_r_on_scalar + [u_bank(s) for s in range(TILES)])
        signed = []

        def spread_vectors(late_bank):
            nc.vector.tensor_copy(out=late_cols[:], in_=late_bank[:, 0:56].bitcast(BF16))
            for b in range(2):
                nc.vector.tensor_tensor(
                    out=rank_scale[:, 4 * b : 4 * b + 4],
                    in0=late_cols[:, 96 + 8 * b : 100 + 8 * b],
                    in1=late_cols[:, 100 + 8 * b : 104 + 8 * b],
                    op=ALU.mult,
                )

        def turn_next(stream, turned_banks):
            if stream:
                key, half = stream.pop(0)
                on_scalar = turned_banks is scalar_turned
                if key[0] == "late":
                    bank[(key, half)] = turn_banks.tile([P, 512], F32, name="turn")
                    nc.tensor.transpose(out=bank[(key, half)][:, 0:P], in_=late_rows[:].bitcast(F32), identity=identity[:])
                else:
                    transpose_half(key, half, weight_banks if on_scalar else turn_banks, "weights" if on_scalar else "turn")
                turned_banks.append((key, half))

        scalar_turned = []
        vector_turned = []

        def next_on_scalar(engine="scalar"):
            if scalar_turned:
                (kind, b, c), half = scalar_turned.pop(0)
                if kind == "v":
                    sign_v(b, c, half, engine)
                else:
                    sign_u(4 * c + 2 * half + b, engine)
                signed.append(((kind, b, c), half))
                turn_next(scalar_banks, scalar_turned)

        def next_on_vector():
            (kind, b, c), half = vector_turned.pop(0)
            if kind == "v":
                sign_v(b, c, half, "vector")
                signed.append(((kind, b, c), half))
            elif kind == "x":
                scale_x(c, half)
            else:
                spread_vectors(bank[((kind, b, c), half)])
            turn_next(vector_banks, vector_turned)
            if vector_turned and vector_turned[0][0][0] == "late":
                next_on_vector()

        def signs_of(b, c):
            for half in range(2):
                while (("v", b, c), half) not in signed:
                    if (("v", b, c), half) in vector_turned + vector_banks:
                        next_on_vector()
                    else:
                        next_on_scalar()

        for i in range(2):
            turn_next(vector_banks, vector_turned)
            turn_next(scalar_banks, scalar_turned)
        for c in range(PASSES):
            next_on_scalar()
            next_on_vector()
            for r in (0, 1):
                stage1_pass(0, c - 2, r)
            next_on_scalar()
            next_on_vector()
            for r in (2, 3):
                stage1_pass(0, c - 2, r)
            quantise_stage1(0, c - 1)
            for i in range(1 if c > 1 else 0):
                next_on_scalar()

        quantise_stage1(0, PASSES - 1)
        for r in range(4):
            stage1_pass(0, PASSES - 2, r)
        signs_of(1, 0)
        next_on_scalar()
        quantise_stage1(1, 0)
        for r in range(4):
            stage1_pass(0, PASSES - 1, r)
        next_on_scalar()
        signs_of(1, 1)
        quantise_stage1(1, 1)
        for r in range(4):
            scale_h(0, r, "scalar")
        for c in range(PASSES):
            if c + 2 < PASSES:
                signs_of(1, c + 2)
                quantise_stage1(1, c + 2)
            for r in range(4):
                stage1_pass(1, c, r)
            if c > 3:
                next_on_scalar()
            if c == 2:
                group_g(0, "vector")
            if c == 2 + 2:
                quantise_g(0)
        for r in range(4):
            scale_h(1, r, ("vector", "scalar")[r % 2])
        for i in range(1):
            next_on_scalar()
        quantised = 0
        quantise_u(0)
        quantise_u(1)
        group_g(1, "vector")
        stage2_pass(0, 0)
        stage2_pass(1, 0)
        quantised = 2
        while u_bank(quantised + 1) in signed:
            quantise_u(quantised)
            quantised += 1
        quantise_g(1)

        for s in range(PAIRS + 3):
            pair = 2 * s
            while quantised < TILES and u_bank(quantised) in signed:
                quantise_u(quantised)
                quantised += 1
            scale_main(pair)
            scale_main(pair + 1)
            add_residual(pair - 2)
            add_residual(pair - 1)
            turn_back(pair - 4)
            turn_back(pair - 3)
            for q, b in ((pair + 2, 0), (pair + 3, 0), (pair, 1), (pair + 1, 1)):
                stage2_pass(q, b)
            next_on_scalar("vector" if s % 2 else "scalar")
            next_on_scalar("vector")
            store(pair - 4, "scalar")
            store(pair - 3, "vector" if not scalar_turned else "scalar")
